import numpy as np
import ml_dtypes


def mxq(x, axis, fmt="e4m3"):
    dtype, down = {"e4m3": (ml_dtypes.float8_e4m3fn, 7), "e5m2": (ml_dtypes.float8_e5m2, 14)}[fmt]
    v = np.moveaxis(np.asarray(x, np.float32).astype(ml_dtypes.bfloat16).astype(np.float64), axis, -1)
    blocks = v.reshape(v.shape[:-1] + (-1, 32))
    amax = np.abs(blocks).max(-1, keepdims=True)
    byte = np.maximum(np.where(amax > 0, np.frexp(amax)[1] - 1 + 127, 0) - down, 1)
    scale = np.exp2(byte - 127.0)
    codes = (blocks / scale).astype(np.float32).astype(dtype).astype(np.float64)
    return np.moveaxis((codes * scale).reshape(v.shape), -1, axis)


WIDE = False


def mx_kscale(k):
    if not WIDE:
        return np.ones(k)
    levels = np.array([10, -10, 5, -5, 0])
    a = np.random.permutation(np.resize(levels, k // 512 * 4)).reshape(k // 512, 4)
    idx = np.arange(k)
    return np.exp2(a[idx // 512, idx % 128 // 32])


BF16 = ml_dtypes.bfloat16


def bf(x):
    return np.asarray(x, np.float32).astype(BF16)


def f64(x):
    return np.asarray(x).astype(np.float64)


E2M1 = np.array([0.0, 0.5, 1.0, 1.5, 2.0, 3.0, 4.0, 6.0, -0.0, -0.5, -1.0, -1.5, -2.0, -3.0, -4.0, -6.0])


def pack_weight(w, fmt):
    k, n = w.shape
    w = f64(bf(w)).reshape(k // 32, 32, n)
    amax = np.abs(w).max(1)
    if fmt == "e4m3":
        byte = np.frexp(amax)[1] - 1 + 127 - 7
    else:
        mant, ex = np.frexp(amax / 6.0)
        byte = np.where(mant > 0.5, ex, ex - 1) + 127
    byte = np.clip(np.where(amax > 0, byte, 1), 1, 254)
    scaled = (w * np.exp2(127.0 - byte)[:, None, :]).reshape(k, n).astype(np.float32)
    by_word = np.ascontiguousarray(scaled.reshape(k // 512, 128, 4, n).transpose(0, 1, 3, 2))
    if fmt == "e4m3":
        words = by_word.astype(ml_dtypes.float8_e4m3fn).view(np.uint8)
    else:
        c = by_word.astype(ml_dtypes.float4_e2m1fn).view(np.uint8) & 0xF
        words = c[..., 0::2] | (c[..., 1::2] << 4)
    return np.ascontiguousarray(words), np.ascontiguousarray(byte.astype(np.uint8).reshape(k // 512, 16, n))


def unpack_weight(words, scales, fmt):
    g, p, n, _ = words.shape
    if fmt == "e4m3":
        vals = np.ascontiguousarray(words).view(ml_dtypes.float8_e4m3fn).astype(np.float64)
    else:
        nib = np.empty((g, p, n, 4), np.uint8)
        nib[..., 0::2] = words & 0xF
        nib[..., 1::2] = words >> 4
        vals = E2M1[nib]
    vals = vals * np.repeat(np.exp2(scales.astype(np.float64) - 127.0), 8, axis=1)[..., None]
    return vals.transpose(0, 1, 3, 2).reshape(g * 512, n)

def pack4(w):
    words, scales = pack_weight(w, "e2m1")
    return words.reshape(words.shape[0], 128, -1), scales


def unpack4(words, scales):
    return unpack_weight(words.reshape(words.shape[0], 128, -1, 2), scales, "e2m1")


B, D0, D1, D2, D3 = 8192, 2048, 2048, 1024, 512
HEBB = 0.01
RATE = 0.001
BATCH_NUM = 1
C = HEBB * RATE / BATCH_NUM


def centred(s):
    return s / np.exp2(np.round(np.log2(s.mean())))


def setup_inputs():
    s = centred(mx_kscale(D2))
    vi = bf(np.maximum(3.0 + 5.0 * np.random.standard_normal((B, D2)), 0.0) * s)
    w = np.random.standard_normal((D3, D2)) * 0.9 / np.sqrt(D2) / s[None, :]
    words, scales = pack4(w.T)
    b = bf(3.0 + 1.5 * np.random.standard_normal(D3))
    return {"vi": vi, "W_words": words, "W_scales": scales, "b": b}


def reference(vi, W_words, W_scales, b):
    vi = f64(vi)
    vj = np.maximum((mxq(vi, 1, "e4m3") @ unpack4(W_words, W_scales)) + f64(b), 0.0)
    m = np.mean(vj, axis=0)
    out = vj + np.sum(vi, axis=1, keepdims=True) * (C * m)[None, :]
    return out, m

@@ -1,0 +1,223 @@
+from contextlib import ExitStack
+
+import concourse.mybir as mybir
+from concourse.masks import make_identity
+
+F32 = mybir.dt.float32
+BF16 = mybir.dt.bfloat16
+I32 = mybir.dt.int32
+U32 = mybir.dt.uint32
+U8 = mybir.dt.uint8
+FP8X4 = mybir.dt.float8_e4m3fn_x4
+FP4X4 = mybir.dt.float4_e2m1fn_x4
+ALU = mybir.AluOpType
+ACT = mybir.ActivationFunctionType
+
+P = 128
+ROWS, K, OUTS = 8192, 1024, 512
+PACK = 4
+K_PASS = P * PACK
+PASSES = K // K_PASS
+TILES = ROWS // P
+UNIT_TILES = 4
+UNIT_ROWS = UNIT_TILES * P
+UNITS = TILES // UNIT_TILES
+OUT_CHUNKS = OUTS // P
+WORDS = K // 2
+C = 0.01 * 0.001 / 1
+
+FLOPS = 2 * ROWS * K * OUTS
+
+
+def tile_optimalnet_pb_t_kernel(tc, vi, W_words, W_scales, b, out_0, out_1):
+    nc = tc.nc
+    vi_tiles = vi.rearrange("(p t) k -> p t k", t=TILES)
+    out_tiles = out_0.rearrange("(p t) o -> p t o", t=TILES)
+
+    with ExitStack() as stack:
+        const = stack.enter_context(tc.tile_pool(name="const", bufs=1))
+        keep = stack.enter_context(tc.tile_pool(name="keep", bufs=1))
+        raw_pool = stack.enter_context(tc.tile_pool(name="raw", bufs=3))
+        work = stack.enter_context(tc.tile_pool(name="work", bufs=2))
+        store_pool = stack.enter_context(tc.tile_pool(name="store", bufs=3))
+        psum = stack.enter_context(tc.psum_pool(name="psum", bufs=4))
+        stack.enter_context(tc.manual_schedule())
+
+        x_raw = {}
+        x_sorted = {}
+        grouped = {}
+        codes = {}
+        vj_t = {}
+
+        def load(u):
+            x_raw[u] = raw_pool.tile([P, UNIT_TILES, K], BF16, name="x_raw")
+            nc.sync.dma_start(
+                out=x_raw[u][:], in_=vi_tiles[:, u * UNIT_TILES : (u + 1) * UNIT_TILES, :]
+            )
+
+        load(0)
+
+        w_words = const.tile([P, PASSES, 2 * OUTS], U8, align_bytes=64)
+        nc.sync.dma_start(
+            out=w_words[:].bitcast(I32), in_=W_words.bitcast(I32).rearrange("g p w -> p g w")
+        )
+        w_scales = const.tile([P, PASSES, OUTS], U8, align_bytes=64)
+        nc.vector.memset(w_scales[:].bitcast(I32), 0)
+        for quad in range(4):
+            nc.sync.dma_start(
+                out=w_scales[32 * quad : 32 * quad + 4, :, :].bitcast(I32),
+                in_=W_scales.bitcast(I32)[:, 4 * quad : 4 * quad + 4, :].rearrange(
+                    "g r w -> r g w"
+                ),
+            )
+        b_rows = const.tile([P, P], BF16)
+        nc.vector.memset(b_rows[:], 0.0)
+        nc.sync.dma_start(out=b_rows[0:OUT_CHUNKS, :], in_=b.rearrange("(c o) -> c o", o=P))
+        load(1)
+        load(2)
+
+        ident = const.tile([P, P], F32)
+        make_identity(nc, ident[:])
+        zeros = const.tile([P, UNIT_ROWS], F32)
+        nc.vector.memset(zeros[:], 0.0)
+        b_rows_f32 = const.tile([P, P], F32)
+        nc.scalar.copy(out=b_rows_f32[:], in_=b_rows[:])
+        b_ps = psum.tile([P, OUTS], F32, tag="acc")
+        nc.tensor.transpose(b_ps[:, 0:P], b_rows_f32[:], ident[:])
+        b_col = const.tile([P, OUT_CHUNKS], F32)
+        nc.scalar.copy(out=b_col[:], in_=b_ps[:, 0:OUT_CHUNKS])
+
+        row_sum = const.tile([P, TILES], F32)
+        col_sum = const.tile([P, OUT_CHUNKS, UNITS], F32)
+
+        def sort_and_sum(u):
+            x_sorted[u] = work.tile([P, UNIT_TILES, K], BF16, name="x_sorted")
+            for j in range(UNIT_TILES):
+                t = u * UNIT_TILES + j
+                nc.vector.tensor_scalar(
+                    out=x_sorted[u][:, j, :].rearrange("p (h q e) -> p h q e", h=2, e=2),
+                    in0=x_raw[u][:, j, :].rearrange("p (q h e) -> p h q e", h=2, e=2),
+                    scalar1=1.0,
+                    scalar2=None,
+                    op0=ALU.mult,
+                    op1=ALU.add,
+                    accum_out=row_sum[:, t : t + 1],
+                )
+
+        def transpose_in(u):
+            grouped[u] = work.tile([P, PASSES, UNIT_ROWS * PACK], BF16, name="grouped", align_bytes=64)
+            for g in range(PASSES):
+                words_g = grouped[u][:, g, :].bitcast(F32).rearrange("p (r h) -> p r h", h=2)
+                for half in range(2):
+                    xt = psum.tile([P, 2, 2 * P], F32, tag="xt")
+                    for jj in range(2):
+                        words = x_sorted[u][:, 2 * half + jj, :].bitcast(F32)
+                        for h in range(2):
+                            first = h * (WORDS // 2) + g * P
+                            nc.tensor.transpose(
+                                xt[:, h, jj * P : (jj + 1) * P], words[:, first : first + P], ident[:]
+                            )
+                    nc.scalar.copy(
+                        out=words_g[:, half * 2 * P : (half + 1) * 2 * P, :],
+                        in_=xt[:].rearrange("p h r -> p r h"),
+                    )
+
+        def quantise(u):
+            words = work.tile([P, PASSES, UNIT_ROWS], U32, name="x_codes", align_bytes=64)
+            scales = work.tile([P, PASSES, UNIT_ROWS], U8, name="x_scales", align_bytes=64)
+            nc.vector.quantize_mx(
+                out=words[:].rearrange("p g r -> p (g r)").bitcast(FP8X4),
+                scales=scales[:].rearrange("p g r -> p (g r)"),
+                in_=grouped[u][:].rearrange("p g c -> p (g c)"),
+            )
+            codes[u] = (words, scales)
+
+        def multiply(u):
+            words, scales = codes[u]
+            vj_t[u] = keep.tile([P, OUT_CHUNKS, UNIT_ROWS], F32, name="vj_t%d" % u)
+            for c in range(OUT_CHUNKS):
+                acc = psum.tile([P, UNIT_ROWS], F32, tag="acc")
+                for g in range(PASSES):
+                    nc.tensor.matmul_mx(
+                        out=acc[:],
+                        lhsT=w_words[:, g, 2 * P * c : 2 * P * (c + 1)].bitcast(FP4X4),
+                        lhsT_scale=w_scales[:, g, P * c : P * (c + 1)],
+                        rhs=words[:, g, :].bitcast(FP8X4),
+                        rhs_scale=scales[:, g, :],
+                        start=(g == 0),
+                        stop=(g == PASSES - 1),
+                    )
+                if c == 0:
+                    nc.vector.scalar_tensor_tensor(
+                        out=vj_t[u][:, c, :],
+                        in0=acc[:],
+                        scalar=b_col[:, c : c + 1],
+                        in1=zeros[:],
+                        op0=ALU.add,
+                        op1=ALU.max,
+                        accum_out=col_sum[:, c, u : u + 1],
+                    )
+                else:
+                    nc.scalar.activation(
+                        out=vj_t[u][:, c, :],
+                        in_=acc[:],
+                        func=ACT.Relu,
+                        bias=b_col[:, c : c + 1],
+                        scale=1.0,
+                        accum_out=col_sum[:, c, u : u + 1],
+                    )
+
+        sort_and_sum(0)
+        transpose_in(0)
+        sort_and_sum(1)
+        quantise(0)
+        for i in range(UNITS):
+            if i + 3 < UNITS:
+                load(i + 3)
+            if i + 2 < UNITS:
+                sort_and_sum(i + 2)
+            if i + 1 < UNITS:
+                transpose_in(i + 1)
+            multiply(i)
+            if i + 1 < UNITS:
+                quantise(i + 1)
+
+        row_factor = const.tile([P, TILES], F32)
+        nc.scalar.mul(out=row_factor[:], in_=row_sum[:], mul=C)
+        total = const.tile([P, OUT_CHUNKS], F32)
+        nc.vector.tensor_reduce(out=total[:], in_=col_sum[:], axis=mybir.AxisListType.X, op=ALU.add)
+        repeated = const.tile([P, OUT_CHUNKS, P], F32)
+        nc.vector.tensor_scalar(
+            out=repeated[:],
+            in0=total[:].unsqueeze(2).to_broadcast([P, OUT_CHUNKS, P]),
+            scalar1=1.0 / ROWS,
+            scalar2=None,
+            op0=ALU.mult,
+        )
+        m_ps = psum.tile([P, OUTS], F32, tag="xt")
+        for c in range(OUT_CHUNKS):
+            nc.tensor.transpose(m_ps[:, c * P : (c + 1) * P], repeated[:, c, :], ident[:])
+        m_all = const.tile([P, OUTS], F32)
+        nc.scalar.copy(out=m_all[:], in_=m_ps[:])
+        nc.sync.dma_start(out=out_1.rearrange("(a o) -> a o", a=1), in_=m_all[0:1, :])
+
+        for u in range(UNITS):
+            result = store_pool.tile([P, UNIT_TILES, OUTS], F32, name="result")
+            for j in range(UNIT_TILES):
+                t = u * UNIT_TILES + j
+                vj = psum.tile([P, OUTS], F32, tag="acc")
+                for c in range(OUT_CHUNKS):
+                    nc.tensor.transpose(
+                        vj[:, c * P : (c + 1) * P], vj_t[u][:, c, j * P : (j + 1) * P], ident[:]
+                    )
+                nc.vector.scalar_tensor_tensor(
+                    out=result[:, j, :],
+                    in0=m_all[:],
+                    scalar=row_factor[:, t : t + 1],
+                    in1=vj[:],
+                    op0=ALU.mult,
+                    op1=ALU.add,
+                )
+            nc.sync.dma_start(
+                out=out_tiles[:, u * UNIT_TILES : (u + 1) * UNIT_TILES, :], in_=result[:]
+            )

@@ -22,6 +22,7 @@ TILES = ROWS // P
 UNIT_TILES = 4
 UNIT_ROWS = UNIT_TILES * P
 UNITS = TILES // UNIT_TILES
+STORE_TILES = 2
 OUT_CHUNKS = OUTS // P
 WORDS = K // 2
 C = 0.01 * 0.001 / 1
@@ -36,10 +37,9 @@ def tile_optimalnet_pb_t_kernel(tc, vi, W_words, W_scales, b, out_0, out_1):
 
     with ExitStack() as stack:
         const = stack.enter_context(tc.tile_pool(name="const", bufs=1))
-        keep = stack.enter_context(tc.tile_pool(name="keep", bufs=1))
+        keep = stack.enter_context(tc.tile_pool(name="keep", bufs=UNITS + 2))
         raw_pool = stack.enter_context(tc.tile_pool(name="raw", bufs=3))
         work = stack.enter_context(tc.tile_pool(name="work", bufs=2))
-        store_pool = stack.enter_context(tc.tile_pool(name="store", bufs=3))
         psum = stack.enter_context(tc.psum_pool(name="psum", bufs=4))
         stack.enter_context(tc.manual_schedule())
 
@@ -51,11 +51,14 @@ def tile_optimalnet_pb_t_kernel(tc, vi, W_words, W_scales, b, out_0, out_1):
 
         def load(u):
             x_raw[u] = raw_pool.tile([P, UNIT_TILES, K], BF16, name="x_raw")
-            nc.sync.dma_start(
-                out=x_raw[u][:], in_=vi_tiles[:, u * UNIT_TILES : (u + 1) * UNIT_TILES, :]
-            )
+            for j in range(UNIT_TILES):
+                nc.sync.dma_start(out=x_raw[u][:, j, :], in_=vi_tiles[:, u * UNIT_TILES + j, :])
 
         load(0)
+
+        b_rows = const.tile([P, P], BF16)
+        nc.vector.memset(b_rows[:], 0.0)
+        nc.scalar.dma_start(out=b_rows[0:OUT_CHUNKS, :], in_=b.rearrange("(c o) -> c o", o=P))
 
         w_words = const.tile([P, PASSES, 2 * OUTS], U8, align_bytes=64)
         nc.sync.dma_start(
@@ -70,9 +73,6 @@ def tile_optimalnet_pb_t_kernel(tc, vi, W_words, W_scales, b, out_0, out_1):
                     "g r w -> r g w"
                 ),
             )
-        b_rows = const.tile([P, P], BF16)
-        nc.vector.memset(b_rows[:], 0.0)
-        nc.sync.dma_start(out=b_rows[0:OUT_CHUNKS, :], in_=b.rearrange("(c o) -> c o", o=P))
         load(1)
         load(2)
 
@@ -80,15 +80,17 @@ def tile_optimalnet_pb_t_kernel(tc, vi, W_words, W_scales, b, out_0, out_1):
         make_identity(nc, ident[:])
         zeros = const.tile([P, UNIT_ROWS], F32)
         nc.vector.memset(zeros[:], 0.0)
-        b_rows_f32 = const.tile([P, P], F32)
-        nc.scalar.copy(out=b_rows_f32[:], in_=b_rows[:])
-        b_ps = psum.tile([P, OUTS], F32, tag="acc")
-        nc.tensor.transpose(b_ps[:, 0:P], b_rows_f32[:], ident[:])
         b_col = const.tile([P, OUT_CHUNKS], F32)
-        nc.scalar.copy(out=b_col[:], in_=b_ps[:, 0:OUT_CHUNKS])
 
         row_sum = const.tile([P, TILES], F32)
         col_sum = const.tile([P, OUT_CHUNKS, UNITS], F32)
+
+        def bias_to_partitions():
+            b_rows_f32 = const.tile([P, P], F32)
+            nc.scalar.copy(out=b_rows_f32[:], in_=b_rows[:])
+            b_ps = psum.tile([P, OUTS], F32, tag="acc")
+            nc.tensor.transpose(b_ps[:, 0:P], b_rows_f32[:], ident[:])
+            nc.scalar.copy(out=b_col[:], in_=b_ps[:, 0:OUT_CHUNKS])
 
         def sort_and_sum(u):
             x_sorted[u] = work.tile([P, UNIT_TILES, K], BF16, name="x_sorted")
@@ -134,7 +136,7 @@ def tile_optimalnet_pb_t_kernel(tc, vi, W_words, W_scales, b, out_0, out_1):
 
         def multiply(u):
             words, scales = codes[u]
-            vj_t[u] = keep.tile([P, OUT_CHUNKS, UNIT_ROWS], F32, name="vj_t%d" % u)
+            vj_t[u] = keep.tile([P, OUT_CHUNKS, UNIT_ROWS], F32, name="vj_t", tag="unit_f32")
             for c in range(OUT_CHUNKS):
                 acc = psum.tile([P, UNIT_ROWS], F32, tag="acc")
                 for g in range(PASSES):
@@ -169,6 +171,7 @@ def tile_optimalnet_pb_t_kernel(tc, vi, W_words, W_scales, b, out_0, out_1):
 
         sort_and_sum(0)
         transpose_in(0)
+        bias_to_partitions()
         sort_and_sum(1)
         quantise(0)
         for i in range(UNITS):
@@ -181,6 +184,47 @@ def tile_optimalnet_pb_t_kernel(tc, vi, W_words, W_scales, b, out_0, out_1):
             multiply(i)
             if i + 1 < UNITS:
                 quantise(i + 1)
+
+        banks = {}
+        results = {}
+
+        def transpose_back(t):
+            u, j = divmod(t, UNIT_TILES)
+            banks[t] = psum.tile([P, OUTS], F32, name="vj", tag="xt" if t % 2 == 0 else "acc")
+            for c in range(OUT_CHUNKS):
+                nc.tensor.transpose(
+                    banks[t][:, c * P : (c + 1) * P], vj_t[u][:, c, j * P : (j + 1) * P], ident[:]
+                )
+
+        def correct_and_store(t):
+            u, j = divmod(t, UNIT_TILES)
+            if j == 0:
+                results[u] = keep.tile([P, UNIT_TILES, OUTS], F32, name="result", tag="unit_f32")
+                correction = work.tile([P, OUTS], F32, name="correction")
+                nc.scalar.activation(
+                    out=correction[:], in_=m_all[:], func=ACT.Copy, scale=row_factor[:, t : t + 1]
+                )
+                nc.scalar.copy(out=results[u][:, j, :], in_=banks[t][:])
+                nc.gpsimd.tensor_tensor(
+                    out=results[u][:, j, :], in0=results[u][:, j, :], in1=correction[:], op=ALU.add
+                )
+            else:
+                nc.vector.scalar_tensor_tensor(
+                    out=results[u][:, j, :],
+                    in0=m_all[:],
+                    scalar=row_factor[:, t : t + 1],
+                    in1=banks[t][:],
+                    op0=ALU.mult,
+                    op1=ALU.add,
+                )
+            if (j + 1) % STORE_TILES == 0:
+                nc.sync.dma_start(
+                    out=out_tiles[:, t + 1 - STORE_TILES : t + 1, :],
+                    in_=results[u][:, j + 1 - STORE_TILES : j + 1, :],
+                )
+
+        for t in range(UNIT_TILES):
+            transpose_back(t)
 
         row_factor = const.tile([P, TILES], F32)
         nc.scalar.mul(out=row_factor[:], in_=row_sum[:], mul=C)
@@ -201,23 +245,7 @@ def tile_optimalnet_pb_t_kernel(tc, vi, W_words, W_scales, b, out_0, out_1):
         nc.scalar.copy(out=m_all[:], in_=m_ps[:])
         nc.sync.dma_start(out=out_1.rearrange("(a o) -> a o", a=1), in_=m_all[0:1, :])
 
-        for u in range(UNITS):
-            result = store_pool.tile([P, UNIT_TILES, OUTS], F32, name="result")
-            for j in range(UNIT_TILES):
-                t = u * UNIT_TILES + j
-                vj = psum.tile([P, OUTS], F32, tag="acc")
-                for c in range(OUT_CHUNKS):
-                    nc.tensor.transpose(
-                        vj[:, c * P : (c + 1) * P], vj_t[u][:, c, j * P : (j + 1) * P], ident[:]
-                    )
-                nc.vector.scalar_tensor_tensor(
-                    out=result[:, j, :],
-                    in0=m_all[:],
-                    scalar=row_factor[:, t : t + 1],
-                    in1=vj[:],
-                    op0=ALU.mult,
-                    op1=ALU.add,
-                )
-            nc.sync.dma_start(
-                out=out_tiles[:, u * UNIT_TILES : (u + 1) * UNIT_TILES, :], in_=result[:]
-            )
+        for t in range(TILES):
+            if t + UNIT_TILES < TILES:
+                transpose_back(t + UNIT_TILES)
+            correct_and_store(t)

@@ -23,6 +23,7 @@ UNIT_TILES = 4
 UNIT_ROWS = UNIT_TILES * P
 UNITS = TILES // UNIT_TILES
 STORE_TILES = 2
+LOOKAHEAD = 6
 OUT_CHUNKS = OUTS // P
 WORDS = K // 2
 C = 0.01 * 0.001 / 1
@@ -192,14 +193,19 @@ def tile_optimalnet_pb_t_kernel(tc, vi, W_words, W_scales, b, out_0, out_1):
             u, j = divmod(t, UNIT_TILES)
             banks[t] = psum.tile([P, OUTS], F32, name="vj", tag="xt" if t % 2 == 0 else "acc")
             for c in range(OUT_CHUNKS):
-                nc.tensor.transpose(
-                    banks[t][:, c * P : (c + 1) * P], vj_t[u][:, c, j * P : (j + 1) * P], ident[:]
-                )
+                block = vj_t[u][:, c, j * P : (j + 1) * P]
+                if c == 0:
+                    nc.tensor.matmul(
+                        banks[t][:, c * P : (c + 1) * P], lhsT=block, rhs=ident[:], start=True, stop=True
+                    )
+                else:
+                    nc.tensor.transpose(banks[t][:, c * P : (c + 1) * P], block, ident[:])
 
         def correct_and_store(t):
             u, j = divmod(t, UNIT_TILES)
             if j == 0:
                 results[u] = keep.tile([P, UNIT_TILES, OUTS], F32, name="result", tag="unit_f32")
+            if j == UNIT_TILES - 1:
                 correction = work.tile([P, OUTS], F32, name="correction")
                 nc.scalar.activation(
                     out=correction[:], in_=m_all[:], func=ACT.Copy, scale=row_factor[:, t : t + 1]
@@ -223,7 +229,7 @@ def tile_optimalnet_pb_t_kernel(tc, vi, W_words, W_scales, b, out_0, out_1):
                     in_=results[u][:, j + 1 - STORE_TILES : j + 1, :],
                 )
 
-        for t in range(UNIT_TILES):
+        for t in range(LOOKAHEAD):
             transpose_back(t)
 
         row_factor = const.tile([P, TILES], F32)
@@ -246,6 +252,6 @@ def tile_optimalnet_pb_t_kernel(tc, vi, W_words, W_scales, b, out_0, out_1):
         nc.sync.dma_start(out=out_1.rearrange("(a o) -> a o", a=1), in_=m_all[0:1, :])
 
         for t in range(TILES):
-            if t + UNIT_TILES < TILES:
-                transpose_back(t + UNIT_TILES)
+            if t + LOOKAHEAD < TILES:
+                transpose_back(t + LOOKAHEAD)
             correct_and_store(t)

@@ -22,6 +22,7 @@ TILES = ROWS // P
 UNIT_TILES = 4
 UNIT_ROWS = UNIT_TILES * P
 UNITS = TILES // UNIT_TILES
+SORTED_TILES = 3
 STORE_TILES = 2
 LOOKAHEAD = 6
 OUT_CHUNKS = OUTS // P
@@ -97,9 +98,15 @@ def tile_optimalnet_pb_t_kernel(tc, vi, W_words, W_scales, b, out_0, out_1):
             x_sorted[u] = work.tile([P, UNIT_TILES, K], BF16, name="x_sorted")
             for j in range(UNIT_TILES):
                 t = u * UNIT_TILES + j
+                if j < SORTED_TILES:
+                    sorted_view = x_sorted[u][:, j, :].rearrange("p (h q e) -> p h q e", h=2, e=2)
+                    raw_view = x_raw[u][:, j, :].rearrange("p (q h e) -> p h q e", h=2, e=2)
+                else:
+                    sorted_view = x_sorted[u][:, j, :]
+                    raw_view = x_raw[u][:, j, :]
                 nc.vector.tensor_scalar(
-                    out=x_sorted[u][:, j, :].rearrange("p (h q e) -> p h q e", h=2, e=2),
-                    in0=x_raw[u][:, j, :].rearrange("p (q h e) -> p h q e", h=2, e=2),
+                    out=sorted_view,
+                    in0=raw_view,
                     scalar1=1.0,
                     scalar2=None,
                     op0=ALU.mult,
@@ -114,12 +121,16 @@ def tile_optimalnet_pb_t_kernel(tc, vi, W_words, W_scales, b, out_0, out_1):
                 for half in range(2):
                     xt = psum.tile([P, 2, 2 * P], F32, tag="xt")
                     for jj in range(2):
-                        words = x_sorted[u][:, 2 * half + jj, :].bitcast(F32)
+                        j = 2 * half + jj
                         for h in range(2):
-                            first = h * (WORDS // 2) + g * P
-                            nc.tensor.transpose(
-                                xt[:, h, jj * P : (jj + 1) * P], words[:, first : first + P], ident[:]
-                            )
+                            if j < SORTED_TILES:
+                                first = h * (WORDS // 2) + g * P
+                                block = x_sorted[u][:, j, :].bitcast(F32)[:, first : first + P]
+                            else:
+                                block = x_raw[u][:, j, :].bitcast(F32)[
+                                    :, 2 * P * g + h : 2 * P * (g + 1) : 2
+                                ]
+                            nc.tensor.transpose(xt[:, h, jj * P : (jj + 1) * P], block, ident[:])
                     nc.scalar.copy(
                         out=words_g[:, half * 2 * P : (half + 1) * 2 * P, :],
                         in_=xt[:].rearrange("p h r -> p r h"),

@@ -39,22 +39,26 @@ def tile_optimalnet_pb_t_kernel(tc, vi, W_words, W_scales, b, out_0, out_1):
 
     with ExitStack() as stack:
         const = stack.enter_context(tc.tile_pool(name="const", bufs=1))
-        keep = stack.enter_context(tc.tile_pool(name="keep", bufs=UNITS + 2))
+        keep = stack.enter_context(tc.tile_pool(name="keep", bufs=UNITS))
+        held_pool = stack.enter_context(tc.tile_pool(name="held", bufs=UNITS))
         raw_pool = stack.enter_context(tc.tile_pool(name="raw", bufs=3))
         work = stack.enter_context(tc.tile_pool(name="work", bufs=2))
         psum = stack.enter_context(tc.psum_pool(name="psum", bufs=4))
         stack.enter_context(tc.manual_schedule())
 
         x_raw = {}
+        held = {}
         x_sorted = {}
         grouped = {}
         codes = {}
         vj_t = {}
 
         def load(u):
-            x_raw[u] = raw_pool.tile([P, UNIT_TILES, K], BF16, name="x_raw")
-            for j in range(UNIT_TILES):
+            x_raw[u] = raw_pool.tile([P, SORTED_TILES, K], BF16, name="x_raw")
+            held[u] = held_pool.tile([P, K], BF16, name="held")
+            for j in range(SORTED_TILES):
                 nc.sync.dma_start(out=x_raw[u][:, j, :], in_=vi_tiles[:, u * UNIT_TILES + j, :])
+            nc.sync.dma_start(out=held[u][:], in_=vi_tiles[:, u * UNIT_TILES + SORTED_TILES, :])
 
         load(0)
 
@@ -95,23 +99,34 @@ def tile_optimalnet_pb_t_kernel(tc, vi, W_words, W_scales, b, out_0, out_1):
             nc.scalar.copy(out=b_col[:], in_=b_ps[:, 0:OUT_CHUNKS])
 
         def sort_and_sum(u):
-            x_sorted[u] = work.tile([P, UNIT_TILES, K], BF16, name="x_sorted")
-            for j in range(UNIT_TILES):
+            x_sorted[u] = work.tile([P, SORTED_TILES, K], BF16, name="x_sorted")
+            for j in range(SORTED_TILES):
                 t = u * UNIT_TILES + j
-                if j < SORTED_TILES:
-                    sorted_view = x_sorted[u][:, j, :].rearrange("p (h q e) -> p h q e", h=2, e=2)
-                    raw_view = x_raw[u][:, j, :].rearrange("p (q h e) -> p h q e", h=2, e=2)
-                else:
-                    sorted_view = x_sorted[u][:, j, :]
-                    raw_view = x_raw[u][:, j, :]
                 nc.vector.tensor_scalar(
-                    out=sorted_view,
-                    in0=raw_view,
+                    out=x_sorted[u][:, j, :].rearrange("p (h q e) -> p h q e", h=2, e=2),
+                    in0=x_raw[u][:, j, :].rearrange("p (q h e) -> p h q e", h=2, e=2),
                     scalar1=1.0,
                     scalar2=None,
                     op0=ALU.mult,
                     op1=ALU.add,
                     accum_out=row_sum[:, t : t + 1],
+                )
+
+        def sum_held(u, engine):
+            t = u * UNIT_TILES + SORTED_TILES
+            if engine == "vector":
+                nc.vector.tensor_scalar(
+                    out=held[u][:],
+                    in0=held[u][:],
+                    scalar1=1.0,
+                    scalar2=None,
+                    op0=ALU.mult,
+                    op1=ALU.add,
+                    accum_out=row_sum[:, t : t + 1],
+                )
+            else:
+                nc.scalar.activation(
+                    out=held[u][:], in_=held[u][:], func=ACT.Copy, accum_out=row_sum[:, t : t + 1]
                 )
 
         def transpose_in(u):
@@ -127,9 +142,7 @@ def tile_optimalnet_pb_t_kernel(tc, vi, W_words, W_scales, b, out_0, out_1):
                                 first = h * (WORDS // 2) + g * P
                                 block = x_sorted[u][:, j, :].bitcast(F32)[:, first : first + P]
                             else:
-                                block = x_raw[u][:, j, :].bitcast(F32)[
-                                    :, 2 * P * g + h : 2 * P * (g + 1) : 2
-                                ]
+                                block = held[u][:].bitcast(F32)[:, 2 * P * g + h : 2 * P * (g + 1) : 2]
                             nc.tensor.transpose(xt[:, h, jj * P : (jj + 1) * P], block, ident[:])
                     nc.scalar.copy(
                         out=words_g[:, half * 2 * P : (half + 1) * 2 * P, :],
@@ -193,9 +206,14 @@ def tile_optimalnet_pb_t_kernel(tc, vi, W_words, W_scales, b, out_0, out_1):
                 sort_and_sum(i + 2)
             if i + 1 < UNITS:
                 transpose_in(i + 1)
+            if i == UNITS - 2:
+                for u in range(0, 3):
+                    sum_held(u, "vector")
             multiply(i)
             if i + 1 < UNITS:
                 quantise(i + 1)
+        for u in range(3, 6):
+            sum_held(u, "vector")
 
         banks = {}
         results = {}
@@ -219,7 +237,7 @@ def tile_optimalnet_pb_t_kernel(tc, vi, W_words, W_scales, b, out_0, out_1):
             if j == UNIT_TILES - 1:
                 correction = work.tile([P, OUTS], F32, name="correction")
                 nc.scalar.activation(
-                    out=correction[:], in_=m_all[:], func=ACT.Copy, scale=row_factor[:, t : t + 1]
+                    out=correction[:], in_=mc_all[:], func=ACT.Copy, scale=row_sum[:, t : t + 1]
                 )
                 nc.scalar.copy(out=results[u][:, j, :], in_=banks[t][:])
                 nc.gpsimd.tensor_tensor(
@@ -228,8 +246,8 @@ def tile_optimalnet_pb_t_kernel(tc, vi, W_words, W_scales, b, out_0, out_1):
             else:
                 nc.vector.scalar_tensor_tensor(
                     out=results[u][:, j, :],
-                    in0=m_all[:],
-                    scalar=row_factor[:, t : t + 1],
+                    in0=mc_all[:],
+                    scalar=row_sum[:, t : t + 1],
                     in1=banks[t][:],
                     op0=ALU.mult,
                     op1=ALU.add,
@@ -243,8 +261,6 @@ def tile_optimalnet_pb_t_kernel(tc, vi, W_words, W_scales, b, out_0, out_1):
         for t in range(LOOKAHEAD):
             transpose_back(t)
 
-        row_factor = const.tile([P, TILES], F32)
-        nc.scalar.mul(out=row_factor[:], in_=row_sum[:], mul=C)
         total = const.tile([P, OUT_CHUNKS], F32)
         nc.vector.tensor_reduce(out=total[:], in_=col_sum[:], axis=mybir.AxisListType.X, op=ALU.add)
         repeated = const.tile([P, OUT_CHUNKS, P], F32)
@@ -258,6 +274,10 @@ def tile_optimalnet_pb_t_kernel(tc, vi, W_words, W_scales, b, out_0, out_1):
         m_ps = psum.tile([P, OUTS], F32, tag="xt")
         for c in range(OUT_CHUNKS):
             nc.tensor.transpose(m_ps[:, c * P : (c + 1) * P], repeated[:, c, :], ident[:])
+        for u in range(6, 8):
+            sum_held(u, "vector")
+        mc_all = const.tile([P, OUTS], F32)
+        nc.scalar.mul(out=mc_all[:], in_=m_ps[:], mul=C)
         m_all = const.tile([P, OUTS], F32)
         nc.scalar.copy(out=m_all[:], in_=m_ps[:])
         nc.sync.dma_start(out=out_1.rearrange("(a o) -> a o", a=1), in_=m_all[0:1, :])
@@ -265,4 +285,6 @@ def tile_optimalnet_pb_t_kernel(tc, vi, W_words, W_scales, b, out_0, out_1):
         for t in range(TILES):
             if t + LOOKAHEAD < TILES:
                 transpose_back(t + LOOKAHEAD)
+            if t % UNIT_TILES == 0 and t // UNIT_TILES + 8 < UNITS:
+                sum_held(t // UNIT_TILES + 8, "scalar")
             correct_and_store(t)

@@ -207,13 +207,16 @@ def tile_optimalnet_pb_t_kernel(tc, vi, W_words, W_scales, b, out_0, out_1):
             if i + 1 < UNITS:
                 transpose_in(i + 1)
             if i == UNITS - 2:
-                for u in range(0, 3):
-                    sum_held(u, "vector")
+                sum_held(0, "vector")
+                sum_held(1, "vector")
+            if i == UNITS - 1:
+                sum_held(2, "vector")
             multiply(i)
             if i + 1 < UNITS:
                 quantise(i + 1)
-        for u in range(3, 6):
-            sum_held(u, "vector")
+        sum_held(3, "vector")
+        sum_held(4, "vector")
+        sum_held(6, "scalar")
 
         banks = {}
         results = {}
@@ -274,17 +277,17 @@ def tile_optimalnet_pb_t_kernel(tc, vi, W_words, W_scales, b, out_0, out_1):
         m_ps = psum.tile([P, OUTS], F32, tag="xt")
         for c in range(OUT_CHUNKS):
             nc.tensor.transpose(m_ps[:, c * P : (c + 1) * P], repeated[:, c, :], ident[:])
-        for u in range(6, 8):
-            sum_held(u, "vector")
+        sum_held(5, "vector")
         mc_all = const.tile([P, OUTS], F32)
         nc.scalar.mul(out=mc_all[:], in_=m_ps[:], mul=C)
         m_all = const.tile([P, OUTS], F32)
         nc.scalar.copy(out=m_all[:], in_=m_ps[:])
         nc.sync.dma_start(out=out_1.rearrange("(a o) -> a o", a=1), in_=m_all[0:1, :])
 
+        late_sums = {(3 * n) // 2: 7 + n for n in range(UNITS - 7)}
         for t in range(TILES):
             if t + LOOKAHEAD < TILES:
                 transpose_back(t + LOOKAHEAD)
-            if t % UNIT_TILES == 0 and t // UNIT_TILES + 8 < UNITS:
-                sum_held(t // UNIT_TILES + 8, "scalar")
+            if t % UNIT_TILES == 0 and t // UNIT_TILES in late_sums:
+                sum_held(late_sums[t // UNIT_TILES], "scalar")
             correct_and_store(t)

@@ -23,7 +23,7 @@ UNIT_TILES = 4
 UNIT_ROWS = UNIT_TILES * P
 UNITS = TILES // UNIT_TILES
 SORTED_TILES = 3
-STORE_TILES = 2
+SMALL_STORE_UNITS = 2
 LOOKAHEAD = 6
 OUT_CHUNKS = OUTS // P
 WORDS = K // 2
@@ -255,10 +255,10 @@ def tile_optimalnet_pb_t_kernel(tc, vi, W_words, W_scales, b, out_0, out_1):
                     op0=ALU.mult,
                     op1=ALU.add,
                 )
-            if (j + 1) % STORE_TILES == 0:
+            if t in store_sizes:
+                n = store_sizes[t]
                 nc.sync.dma_start(
-                    out=out_tiles[:, t + 1 - STORE_TILES : t + 1, :],
-                    in_=results[u][:, j + 1 - STORE_TILES : j + 1, :],
+                    out=out_tiles[:, t + 1 - n : t + 1, :], in_=results[u][:, j + 1 - n : j + 1, :]
                 )
 
         for t in range(LOOKAHEAD):
@@ -284,6 +284,13 @@ def tile_optimalnet_pb_t_kernel(tc, vi, W_words, W_scales, b, out_0, out_1):
         nc.scalar.copy(out=m_all[:], in_=m_ps[:])
         nc.sync.dma_start(out=out_1.rearrange("(a o) -> a o", a=1), in_=m_all[0:1, :])
 
+        store_sizes = {0: 1, 1: 1, 3: 2}
+        for u in range(1, UNITS):
+            if u < SMALL_STORE_UNITS or u == UNITS - 1:
+                store_sizes[u * UNIT_TILES + 1] = 2
+                store_sizes[u * UNIT_TILES + 3] = 2
+            else:
+                store_sizes[u * UNIT_TILES + 3] = UNIT_TILES
         late_sums = {(3 * n) // 2: 7 + n for n in range(UNITS - 7)}
         for t in range(TILES):
             if t + LOOKAHEAD < TILES:

@@ -216,7 +216,6 @@ def tile_optimalnet_pb_t_kernel(tc, vi, W_words, W_scales, b, out_0, out_1):
                 quantise(i + 1)
         sum_held(3, "vector")
         sum_held(4, "vector")
-        sum_held(6, "scalar")
 
         banks = {}
         results = {}
@@ -261,40 +260,56 @@ def tile_optimalnet_pb_t_kernel(tc, vi, W_words, W_scales, b, out_0, out_1):
                     out=out_tiles[:, t + 1 - n : t + 1, :], in_=results[u][:, j + 1 - n : j + 1, :]
                 )
 
-        for t in range(LOOKAHEAD):
-            transpose_back(t)
-
         total = const.tile([P, OUT_CHUNKS], F32)
-        nc.vector.tensor_reduce(out=total[:], in_=col_sum[:], axis=mybir.AxisListType.X, op=ALU.add)
         repeated = const.tile([P, OUT_CHUNKS, P], F32)
-        nc.vector.tensor_scalar(
-            out=repeated[:],
-            in0=total[:].unsqueeze(2).to_broadcast([P, OUT_CHUNKS, P]),
-            scalar1=1.0 / ROWS,
-            scalar2=None,
-            op0=ALU.mult,
-        )
+
+        def spread_mean(first, last):
+            nc.vector.tensor_reduce(
+                out=total[:, first:last],
+                in_=col_sum[:, first:last, :],
+                axis=mybir.AxisListType.X,
+                op=ALU.add,
+            )
+            nc.vector.tensor_scalar(
+                out=repeated[:, first:last, :],
+                in0=total[:, first:last].unsqueeze(2).to_broadcast([P, last - first, P]),
+                scalar1=1.0 / ROWS,
+                scalar2=None,
+                op0=ALU.mult,
+            )
+            for c in range(first, last):
+                nc.tensor.transpose(m_ps[:, c * P : (c + 1) * P], repeated[:, c, :], ident[:])
+
+        transpose_back(0)
+        transpose_back(1)
         m_ps = psum.tile([P, OUTS], F32, tag="xt")
-        for c in range(OUT_CHUNKS):
-            nc.tensor.transpose(m_ps[:, c * P : (c + 1) * P], repeated[:, c, :], ident[:])
+        spread_mean(0, OUT_CHUNKS - 1)
+        spread_mean(OUT_CHUNKS - 1, OUT_CHUNKS)
+        for t in range(2, LOOKAHEAD):
+            transpose_back(t)
         sum_held(5, "vector")
         mc_all = const.tile([P, OUTS], F32)
         nc.scalar.mul(out=mc_all[:], in_=m_ps[:], mul=C)
         m_all = const.tile([P, OUTS], F32)
         nc.scalar.copy(out=m_all[:], in_=m_ps[:])
-        nc.sync.dma_start(out=out_1.rearrange("(a o) -> a o", a=1), in_=m_all[0:1, :])
 
         store_sizes = {0: 1, 1: 1, 3: 2}
         for u in range(1, UNITS):
-            if u < SMALL_STORE_UNITS or u == UNITS - 1:
+            if u < SMALL_STORE_UNITS:
                 store_sizes[u * UNIT_TILES + 1] = 2
                 store_sizes[u * UNIT_TILES + 3] = 2
-            else:
+            elif u < UNITS - 1:
                 store_sizes[u * UNIT_TILES + 3] = UNIT_TILES
-        late_sums = {(3 * n) // 2: 7 + n for n in range(UNITS - 7)}
-        for t in range(TILES):
+        store_sizes[TILES - 3] = 2
+        store_sizes[TILES - 1] = 1
+        store_sizes[TILES - 2] = 1
+        tile_order = list(range(TILES - 2)) + [TILES - 1, TILES - 2]
+        late_sums = {(3 * n) // 2: 6 + n for n in range(UNITS - 6)}
+        for t in tile_order:
             if t + LOOKAHEAD < TILES:
                 transpose_back(t + LOOKAHEAD)
             if t % UNIT_TILES == 0 and t // UNIT_TILES in late_sums:
                 sum_held(late_sums[t // UNIT_TILES], "scalar")
             correct_and_store(t)
+            if t == UNIT_TILES - 1:
+                nc.sync.dma_start(out=out_1.rearrange("(a o) -> a o", a=1), in_=m_all[0:1, :])

@@ -66,6 +66,8 @@ def tile_optimalnet_pb_t_kernel(tc, vi, W_words, W_scales, b, out_0, out_1):
         nc.vector.memset(b_rows[:], 0.0)
         nc.scalar.dma_start(out=b_rows[0:OUT_CHUNKS, :], in_=b.rearrange("(c o) -> c o", o=P))
 
+        load(1)
+
         w_words = const.tile([P, PASSES, 2 * OUTS], U8, align_bytes=64)
         nc.sync.dma_start(
             out=w_words[:].bitcast(I32), in_=W_words.bitcast(I32).rearrange("g p w -> p g w")
@@ -79,7 +81,6 @@ def tile_optimalnet_pb_t_kernel(tc, vi, W_words, W_scales, b, out_0, out_1):
                     "g r w -> r g w"
                 ),
             )
-        load(1)
         load(2)
 
         ident = const.tile([P, P], F32)
@@ -91,9 +92,9 @@ def tile_optimalnet_pb_t_kernel(tc, vi, W_words, W_scales, b, out_0, out_1):
         row_sum = const.tile([P, TILES], F32)
         col_sum = const.tile([P, OUT_CHUNKS, UNITS], F32)
 
+        b_rows_f32 = const.tile([P, P], F32)
+
         def bias_to_partitions():
-            b_rows_f32 = const.tile([P, P], F32)
-            nc.scalar.copy(out=b_rows_f32[:], in_=b_rows[:])
             b_ps = psum.tile([P, OUTS], F32, tag="acc")
             nc.tensor.transpose(b_ps[:, 0:P], b_rows_f32[:], ident[:])
             nc.scalar.copy(out=b_col[:], in_=b_ps[:, 0:OUT_CHUNKS])
@@ -130,7 +131,7 @@ def tile_optimalnet_pb_t_kernel(tc, vi, W_words, W_scales, b, out_0, out_1):
                 )
 
         def transpose_in(u):
-            grouped[u] = work.tile([P, PASSES, UNIT_ROWS * PACK], BF16, name="grouped", align_bytes=64)
+            grouped[u] = work.tile([P, PASSES, UNIT_ROWS * PACK], BF16, name="grouped", tag="grouped", align_bytes=64)
             for g in range(PASSES):
                 words_g = grouped[u][:, g, :].bitcast(F32).rearrange("p (r h) -> p r h", h=2)
                 for half in range(2):
@@ -152,48 +153,60 @@ def tile_optimalnet_pb_t_kernel(tc, vi, W_words, W_scales, b, out_0, out_1):
         def quantise(u):
             words = work.tile([P, PASSES, UNIT_ROWS], U32, name="x_codes", align_bytes=64)
             scales = work.tile([P, PASSES, UNIT_ROWS], U8, name="x_scales", align_bytes=64)
-            nc.vector.quantize_mx(
-                out=words[:].rearrange("p g r -> p (g r)").bitcast(FP8X4),
-                scales=scales[:].rearrange("p g r -> p (g r)"),
-                in_=grouped[u][:].rearrange("p g c -> p (g c)"),
-            )
+            if u < UNITS - 1:
+                nc.vector.quantize_mx(
+                    out=words[:].rearrange("p g r -> p (g r)").bitcast(FP8X4),
+                    scales=scales[:].rearrange("p g r -> p (g r)"),
+                    in_=grouped[u][:].rearrange("p g c -> p (g c)"),
+                )
+            else:
+                for g in range(PASSES):
+                    nc.vector.quantize_mx(
+                        out=words[:, g, :].bitcast(FP8X4), scales=scales[:, g, :], in_=grouped[u][:, g, :]
+                    )
             codes[u] = (words, scales)
 
         def multiply(u):
             words, scales = codes[u]
             vj_t[u] = keep.tile([P, OUT_CHUNKS, UNIT_ROWS], F32, name="vj_t", tag="unit_f32")
+            acc = {}
             for c in range(OUT_CHUNKS):
-                acc = psum.tile([P, UNIT_ROWS], F32, tag="acc")
-                for g in range(PASSES):
-                    nc.tensor.matmul_mx(
-                        out=acc[:],
-                        lhsT=w_words[:, g, 2 * P * c : 2 * P * (c + 1)].bitcast(FP4X4),
-                        lhsT_scale=w_scales[:, g, P * c : P * (c + 1)],
-                        rhs=words[:, g, :].bitcast(FP8X4),
-                        rhs_scale=scales[:, g, :],
-                        start=(g == 0),
-                        stop=(g == PASSES - 1),
-                    )
-                if c == 0:
+                acc[c] = psum.tile([P, UNIT_ROWS], F32, name="acc", tag="acc")
+            if u < UNITS - 1:
+                steps = [(c, g) for c in range(OUT_CHUNKS) for g in range(PASSES)]
+            else:
+                steps = [(c, g) for g in range(PASSES) for c in range(OUT_CHUNKS)]
+            for c, g in steps:
+                nc.tensor.matmul_mx(
+                    out=acc[c][:],
+                    lhsT=w_words[:, g, 2 * P * c : 2 * P * (c + 1)].bitcast(FP4X4),
+                    lhsT_scale=w_scales[:, g, P * c : P * (c + 1)],
+                    rhs=words[:, g, :].bitcast(FP8X4),
+                    rhs_scale=scales[:, g, :],
+                    start=(g == 0),
+                    stop=(g == PASSES - 1),
+                )
+                if g == PASSES - 1 and (c == 0 or (c == 2 and u == UNITS - 1)):
                     nc.vector.scalar_tensor_tensor(
                         out=vj_t[u][:, c, :],
-                        in0=acc[:],
+                        in0=acc[c][:],
                         scalar=b_col[:, c : c + 1],
                         in1=zeros[:],
                         op0=ALU.add,
                         op1=ALU.max,
                         accum_out=col_sum[:, c, u : u + 1],
                     )
-                else:
+                elif g == PASSES - 1:
                     nc.scalar.activation(
                         out=vj_t[u][:, c, :],
-                        in_=acc[:],
+                        in_=acc[c][:],
                         func=ACT.Relu,
                         bias=b_col[:, c : c + 1],
                         scale=1.0,
                         accum_out=col_sum[:, c, u : u + 1],
                     )
 
+        nc.scalar.copy(out=b_rows_f32[:], in_=b_rows[:])
         sort_and_sum(0)
         transpose_in(0)
         bias_to_partitions()
@@ -211,11 +224,10 @@ def tile_optimalnet_pb_t_kernel(tc, vi, W_words, W_scales, b, out_0, out_1):
                 sum_held(1, "vector")
             if i == UNITS - 1:
                 sum_held(2, "vector")
+                sum_held(3, "vector")
             multiply(i)
             if i + 1 < UNITS:
                 quantise(i + 1)
-        sum_held(3, "vector")
-        sum_held(4, "vector")
 
         banks = {}
         results = {}
@@ -232,33 +244,31 @@ def tile_optimalnet_pb_t_kernel(tc, vi, W_words, W_scales, b, out_0, out_1):
                 else:
                     nc.tensor.transpose(banks[t][:, c * P : (c + 1) * P], block, ident[:])
 
-        def correct_and_store(t):
+        def finish_by_vector(t):
             u, j = divmod(t, UNIT_TILES)
-            if j == 0:
-                results[u] = keep.tile([P, UNIT_TILES, OUTS], F32, name="result", tag="unit_f32")
-            if j == UNIT_TILES - 1:
-                correction = work.tile([P, OUTS], F32, name="correction")
-                nc.scalar.activation(
-                    out=correction[:], in_=mc_all[:], func=ACT.Copy, scale=row_sum[:, t : t + 1]
-                )
-                nc.scalar.copy(out=results[u][:, j, :], in_=banks[t][:])
-                nc.gpsimd.tensor_tensor(
-                    out=results[u][:, j, :], in0=results[u][:, j, :], in1=correction[:], op=ALU.add
-                )
-            else:
-                nc.vector.scalar_tensor_tensor(
-                    out=results[u][:, j, :],
-                    in0=mc_all[:],
-                    scalar=row_sum[:, t : t + 1],
-                    in1=banks[t][:],
-                    op0=ALU.mult,
-                    op1=ALU.add,
-                )
-            if t in store_sizes:
-                n = store_sizes[t]
-                nc.sync.dma_start(
-                    out=out_tiles[:, t + 1 - n : t + 1, :], in_=results[u][:, j + 1 - n : j + 1, :]
-                )
+            nc.vector.scalar_tensor_tensor(
+                out=results[u][:, j, :],
+                in0=mc_all[:],
+                scalar=row_sum[:, t : t + 1],
+                in1=banks[t][:],
+                op0=ALU.mult,
+                op1=ALU.add,
+            )
+
+        def finish_by_scalar_and_gpsimd(t):
+            u, j = divmod(t, UNIT_TILES)
+            correction = work.tile([P, OUTS], F32, name="correction")
+            nc.scalar.activation(
+                out=correction[:], in_=mc_all[:], func=ACT.Copy, scale=row_sum[:, t : t + 1]
+            )
+            nc.scalar.copy(out=results[u][:, j, :], in_=banks[t][:])
+            nc.gpsimd.tensor_tensor(
+                out=results[u][:, j, :], in0=results[u][:, j, :], in1=correction[:], op=ALU.add
+            )
+
+        def store(first, n):
+            u, j = divmod(first, UNIT_TILES)
+            nc.sync.dma_start(out=out_tiles[:, first : first + n, :], in_=results[u][:, j : j + n, :])
 
         total = const.tile([P, OUT_CHUNKS], F32)
         repeated = const.tile([P, OUT_CHUNKS, P], F32)
@@ -277,39 +287,53 @@ def tile_optimalnet_pb_t_kernel(tc, vi, W_words, W_scales, b, out_0, out_1):
                 scalar2=None,
                 op0=ALU.mult,
             )
+            m_ps = psum.tile([P, OUTS], F32, name="m_ps", tag="xt" if first == 0 else "acc")
             for c in range(first, last):
                 nc.tensor.transpose(m_ps[:, c * P : (c + 1) * P], repeated[:, c, :], ident[:])
+            nc.scalar.mul(out=mc_all[:, first * P : last * P], in_=m_ps[:, first * P : last * P], mul=C)
+            return m_ps
 
         transpose_back(0)
         transpose_back(1)
-        m_ps = psum.tile([P, OUTS], F32, tag="xt")
-        spread_mean(0, OUT_CHUNKS - 1)
-        spread_mean(OUT_CHUNKS - 1, OUT_CHUNKS)
+        mc_all = const.tile([P, OUTS], F32)
+        m_first = spread_mean(0, OUT_CHUNKS - 1)
+        m_last = spread_mean(OUT_CHUNKS - 1, OUT_CHUNKS)
         for t in range(2, LOOKAHEAD):
             transpose_back(t)
+        sum_held(4, "vector")
         sum_held(5, "vector")
-        mc_all = const.tile([P, OUTS], F32)
-        nc.scalar.mul(out=mc_all[:], in_=m_ps[:], mul=C)
-        m_all = const.tile([P, OUTS], F32)
-        nc.scalar.copy(out=m_all[:], in_=m_ps[:])
 
-        store_sizes = {0: 1, 1: 1, 3: 2}
+        stores = {0: [(0, 1)], 1: [(1, 1)], 2: [(2, 1), (3, 1)]}
         for u in range(1, UNITS):
+            first = u * UNIT_TILES
             if u < SMALL_STORE_UNITS:
-                store_sizes[u * UNIT_TILES + 1] = 2
-                store_sizes[u * UNIT_TILES + 3] = 2
+                stores[first + 1] = [(first, 2)]
+                stores[first + 2] = [(first + 2, 2)]
             elif u < UNITS - 1:
-                store_sizes[u * UNIT_TILES + 3] = UNIT_TILES
-        store_sizes[TILES - 3] = 2
-        store_sizes[TILES - 1] = 1
-        store_sizes[TILES - 2] = 1
-        tile_order = list(range(TILES - 2)) + [TILES - 1, TILES - 2]
-        late_sums = {(3 * n) // 2: 6 + n for n in range(UNITS - 6)}
-        for t in tile_order:
+                stores[first + 2] = [(first, UNIT_TILES)]
+            else:
+                stores[first + 1] = [(first, 2), (first + 3, 1)]
+                stores[first + 2] = [(first + 2, 1)]
+        late_sums = {(3 * n) // 2 + 1: 6 + n for n in range(UNITS - 6)}
+        for t in range(TILES):
+            u, j = divmod(t, UNIT_TILES)
             if t + LOOKAHEAD < TILES:
                 transpose_back(t + LOOKAHEAD)
-            if t % UNIT_TILES == 0 and t // UNIT_TILES in late_sums:
-                sum_held(late_sums[t // UNIT_TILES], "scalar")
-            correct_and_store(t)
-            if t == UNIT_TILES - 1:
+            if j == 0 and u < 2:
+                results[u] = work.tile([P, UNIT_TILES, OUTS], F32, name="result", tag="grouped", align_bytes=64)
+            elif j == 0:
+                results[u] = keep.tile([P, UNIT_TILES, OUTS], F32, name="result", tag="unit_f32")
+            if j == 0:
+                if u in late_sums:
+                    sum_held(late_sums[u], "scalar")
+                finish_by_scalar_and_gpsimd(t + UNIT_TILES - 1)
+            if j < UNIT_TILES - 1:
+                finish_by_vector(t)
+            for first, n in stores.get(t, []):
+                store(first, n)
+            if t == 1:
+                m_all = const.tile([P, OUTS], F32)
+                split = (OUT_CHUNKS - 1) * P
+                nc.scalar.copy(out=m_all[:, 0:split], in_=m_first[:, 0:split])
+                nc.scalar.copy(out=m_all[:, split:OUTS], in_=m_last[:, split:OUTS])
                 nc.sync.dma_start(out=out_1.rearrange("(a o) -> a o", a=1), in_=m_all[0:1, :])

@@ -22,6 +22,7 @@ TILES = ROWS // P
 UNIT_TILES = 4
 UNIT_ROWS = UNIT_TILES * P
 UNITS = TILES // UNIT_TILES
+LATE_UNITS = 3
 SORTED_TILES = 3
 SMALL_STORE_UNITS = 2
 LOOKAHEAD = 6
@@ -103,6 +104,12 @@ def tile_optimalnet_pb_t_kernel(tc, vi, W_words, W_scales, b, out_0, out_1):
             x_sorted[u] = work.tile([P, SORTED_TILES, K], BF16, name="x_sorted")
             for j in range(SORTED_TILES):
                 t = u * UNIT_TILES + j
+                if u >= UNITS - LATE_UNITS:
+                    nc.vector.tensor_copy(
+                        out=x_sorted[u][:, j, :].bitcast(F32).rearrange("p (h q) -> p h q", h=2),
+                        in_=x_raw[u][:, j, :].bitcast(F32).rearrange("p (q h) -> p h q", h=2),
+                    )
+                    continue
                 nc.vector.tensor_scalar(
                     out=x_sorted[u][:, j, :].rearrange("p (h q e) -> p h q e", h=2, e=2),
                     in0=x_raw[u][:, j, :].rearrange("p (q h e) -> p h q e", h=2, e=2),
@@ -113,12 +120,13 @@ def tile_optimalnet_pb_t_kernel(tc, vi, W_words, W_scales, b, out_0, out_1):
                     accum_out=row_sum[:, t : t + 1],
                 )
 
-        def sum_held(u, engine):
-            t = u * UNIT_TILES + SORTED_TILES
+        def sum_late(t, engine):
+            u, j = divmod(t, UNIT_TILES)
+            rows = x_raw[u][:, j, :] if j < SORTED_TILES else held[u][:]
             if engine == "vector":
                 nc.vector.tensor_scalar(
-                    out=held[u][:],
-                    in0=held[u][:],
+                    out=rows,
+                    in0=rows,
                     scalar1=1.0,
                     scalar2=None,
                     op0=ALU.mult,
@@ -126,9 +134,7 @@ def tile_optimalnet_pb_t_kernel(tc, vi, W_words, W_scales, b, out_0, out_1):
                     accum_out=row_sum[:, t : t + 1],
                 )
             else:
-                nc.scalar.activation(
-                    out=held[u][:], in_=held[u][:], func=ACT.Copy, accum_out=row_sum[:, t : t + 1]
-                )
+                nc.scalar.activation(out=rows, in_=rows, func=ACT.Copy, accum_out=row_sum[:, t : t + 1])
 
         def transpose_in(u):
             grouped[u] = work.tile([P, PASSES, UNIT_ROWS * PACK], BF16, name="grouped", tag="grouped", align_bytes=64)
@@ -220,11 +226,11 @@ def tile_optimalnet_pb_t_kernel(tc, vi, W_words, W_scales, b, out_0, out_1):
             if i + 1 < UNITS:
                 transpose_in(i + 1)
             if i == UNITS - 2:
-                sum_held(0, "vector")
-                sum_held(1, "vector")
+                sum_late(3, "vector")
+                sum_late(7, "vector")
             if i == UNITS - 1:
-                sum_held(2, "vector")
-                sum_held(3, "vector")
+                sum_late(11, "vector")
+                sum_late(15, "vector")
             multiply(i)
             if i + 1 < UNITS:
                 quantise(i + 1)
@@ -300,8 +306,8 @@ def tile_optimalnet_pb_t_kernel(tc, vi, W_words, W_scales, b, out_0, out_1):
         m_last = spread_mean(OUT_CHUNKS - 1, OUT_CHUNKS)
         for t in range(2, LOOKAHEAD):
             transpose_back(t)
-        sum_held(4, "vector")
-        sum_held(5, "vector")
+        sum_late(19, "vector")
+        sum_late(23, "vector")
 
         stores = {0: [(0, 1)], 1: [(1, 1)], 2: [(2, 1), (3, 1)]}
         for u in range(1, UNITS):
@@ -314,7 +320,11 @@ def tile_optimalnet_pb_t_kernel(tc, vi, W_words, W_scales, b, out_0, out_1):
             else:
                 stores[first + 1] = [(first, 2), (first + 3, 1)]
                 stores[first + 2] = [(first + 2, 1)]
-        late_sums = {(3 * n) // 2 + 1: 6 + n for n in range(UNITS - 6)}
+        late_sums = {(3 * n) // 2 + 1: (6 + n) * UNIT_TILES + SORTED_TILES for n in range(UNITS - 6)}
+        unsummed = [
+            u * UNIT_TILES + j for u in range(UNITS - LATE_UNITS, UNITS) for j in range(SORTED_TILES)
+        ]
+        vector_sums = {3 + n: t for n, t in enumerate(unsummed)}
         for t in range(TILES):
             u, j = divmod(t, UNIT_TILES)
             if t + LOOKAHEAD < TILES:
@@ -325,10 +335,12 @@ def tile_optimalnet_pb_t_kernel(tc, vi, W_words, W_scales, b, out_0, out_1):
                 results[u] = keep.tile([P, UNIT_TILES, OUTS], F32, name="result", tag="unit_f32")
             if j == 0:
                 if u in late_sums:
-                    sum_held(late_sums[u], "scalar")
+                    sum_late(late_sums[u], "scalar")
                 finish_by_scalar_and_gpsimd(t + UNIT_TILES - 1)
             if j < UNIT_TILES - 1:
                 finish_by_vector(t)
+            if j == UNIT_TILES - 2 and u in vector_sums:
+                sum_late(vector_sums[u], "vector")
             for first, n in stores.get(t, []):
                 store(first, n)
             if t == 1:

@@ -93,6 +93,9 @@ def tile_optimalnet_pb_t_kernel(tc, vi, W_words, W_scales, b, out_0, out_1):
         row_sum = const.tile([P, TILES], F32)
         col_sum = const.tile([P, OUT_CHUNKS, UNITS], F32)
 
+        partial = const.tile([P, OUT_CHUNKS], F32)
+        repeated = const.tile([P, OUT_CHUNKS, P], F32)
+
         b_rows_f32 = const.tile([P, P], F32)
 
         def bias_to_partitions():
@@ -182,6 +185,14 @@ def tile_optimalnet_pb_t_kernel(tc, vi, W_words, W_scales, b, out_0, out_1):
                 steps = [(c, g) for c in range(OUT_CHUNKS) for g in range(PASSES)]
             else:
                 steps = [(c, g) for g in range(PASSES) for c in range(OUT_CHUNKS)]
+            if u == UNITS - 1:
+                sum_late(19, "vector")
+                nc.vector.tensor_reduce(
+                    out=partial[:], in_=col_sum[:, :, 0:u], axis=mybir.AxisListType.X, op=ALU.add
+                )
+                nc.vector.tensor_scalar(
+                    out=partial[:], in0=partial[:], scalar1=1.0 / ROWS, scalar2=None, op0=ALU.mult
+                )
             for c, g in steps:
                 nc.tensor.matmul_mx(
                     out=acc[c][:],
@@ -202,6 +213,15 @@ def tile_optimalnet_pb_t_kernel(tc, vi, W_words, W_scales, b, out_0, out_1):
                         op1=ALU.max,
                         accum_out=col_sum[:, c, u : u + 1],
                     )
+                    if u == UNITS - 1:
+                        nc.vector.tensor_scalar(
+                            out=repeated[:, c, :],
+                            in0=col_sum[:, c, u : u + 1].to_broadcast([P, P]),
+                            scalar1=1.0 / ROWS,
+                            scalar2=partial[:, c : c + 1],
+                            op0=ALU.mult,
+                            op1=ALU.add,
+                        )
                 elif g == PASSES - 1:
                     nc.scalar.activation(
                         out=vj_t[u][:, c, :],
@@ -211,6 +231,14 @@ def tile_optimalnet_pb_t_kernel(tc, vi, W_words, W_scales, b, out_0, out_1):
                         scale=1.0,
                         accum_out=col_sum[:, c, u : u + 1],
                     )
+                    if u == UNITS - 1:
+                        nc.scalar.activation(
+                            out=repeated[:, c, :],
+                            in_=col_sum[:, c, u : u + 1].to_broadcast([P, P]),
+                            func=ACT.Identity,
+                            bias=partial[:, c : c + 1],
+                            scale=1.0 / ROWS,
+                        )
 
         nc.scalar.copy(out=b_rows_f32[:], in_=b_rows[:])
         sort_and_sum(0)
@@ -228,9 +256,9 @@ def tile_optimalnet_pb_t_kernel(tc, vi, W_words, W_scales, b, out_0, out_1):
             if i == UNITS - 2:
                 sum_late(3, "vector")
                 sum_late(7, "vector")
-            if i == UNITS - 1:
                 sum_late(11, "vector")
-                sum_late(15, "vector")
+            if i == UNITS - 1:
+                sum_late(15, "scalar")
             multiply(i)
             if i + 1 < UNITS:
                 quantise(i + 1)
@@ -240,10 +268,10 @@ def tile_optimalnet_pb_t_kernel(tc, vi, W_words, W_scales, b, out_0, out_1):
 
         def transpose_back(t):
             u, j = divmod(t, UNIT_TILES)
-            banks[t] = psum.tile([P, OUTS], F32, name="vj", tag="xt" if t % 2 == 0 else "acc")
+            banks[t] = psum.tile([P, OUTS], F32, name="vj", tag="xt" if len(banks) % 2 == 0 else "acc")
             for c in range(OUT_CHUNKS):
                 block = vj_t[u][:, c, j * P : (j + 1) * P]
-                if c == 0:
+                if c == 0 and t % 3 != 2:
                     nc.tensor.matmul(
                         banks[t][:, c * P : (c + 1) * P], lhsT=block, rhs=ident[:], start=True, stop=True
                     )
@@ -276,76 +304,67 @@ def tile_optimalnet_pb_t_kernel(tc, vi, W_words, W_scales, b, out_0, out_1):
             u, j = divmod(first, UNIT_TILES)
             nc.sync.dma_start(out=out_tiles[:, first : first + n, :], in_=results[u][:, j : j + n, :])
 
-        total = const.tile([P, OUT_CHUNKS], F32)
-        repeated = const.tile([P, OUT_CHUNKS, P], F32)
-
-        def spread_mean(first, last):
-            nc.vector.tensor_reduce(
-                out=total[:, first:last],
-                in_=col_sum[:, first:last, :],
-                axis=mybir.AxisListType.X,
-                op=ALU.add,
-            )
-            nc.vector.tensor_scalar(
-                out=repeated[:, first:last, :],
-                in0=total[:, first:last].unsqueeze(2).to_broadcast([P, last - first, P]),
-                scalar1=1.0 / ROWS,
-                scalar2=None,
-                op0=ALU.mult,
-            )
-            m_ps = psum.tile([P, OUTS], F32, name="m_ps", tag="xt" if first == 0 else "acc")
-            for c in range(first, last):
-                nc.tensor.transpose(m_ps[:, c * P : (c + 1) * P], repeated[:, c, :], ident[:])
-            nc.scalar.mul(out=mc_all[:, first * P : last * P], in_=m_ps[:, first * P : last * P], mul=C)
-            return m_ps
+        mc_all = const.tile([P, OUTS], F32)
+        order = list(range(UNIT_TILES))
+        for u in range(1, UNITS):
+            order.insert(len(order) - (UNIT_TILES - 1 if u > 1 else 2), u * UNIT_TILES + SORTED_TILES)
+            order.extend(range(u * UNIT_TILES, u * UNIT_TILES + SORTED_TILES))
+        by_gpsimd = set(u * UNIT_TILES + SORTED_TILES for u in range(1, UNITS))
 
         transpose_back(0)
-        transpose_back(1)
-        mc_all = const.tile([P, OUTS], F32)
-        m_first = spread_mean(0, OUT_CHUNKS - 1)
-        m_last = spread_mean(OUT_CHUNKS - 1, OUT_CHUNKS)
-        for t in range(2, LOOKAHEAD):
+        halves = []
+        for half in range(2):
+            m_ps = psum.tile([P, OUTS // 2], F32, name="m_ps", tag="xt" if half == 0 else "acc")
+            for c in range(2):
+                nc.tensor.transpose(m_ps[:, c * P : (c + 1) * P], repeated[:, 2 * half + c, :], ident[:])
+            halves.append(m_ps)
+            if half == 0:
+                transpose_back(order[1])
+        nc.scalar.mul(out=mc_all[:, 0 : OUTS // 2], in_=halves[0][:], mul=C)
+        nc.vector.tensor_scalar(
+            out=mc_all[:, OUTS // 2 : OUTS], in0=halves[1][:], scalar1=C, scalar2=None, op0=ALU.mult
+        )
+        for t in order[2:LOOKAHEAD]:
             transpose_back(t)
-        sum_late(19, "vector")
-        sum_late(23, "vector")
 
-        stores = {0: [(0, 1)], 1: [(1, 1)], 2: [(2, 1), (3, 1)]}
+        stores = {0: [(0, 1)], 1: [(1, 1)], 2: [(2, 1)], 3: [(3, 1)]}
         for u in range(1, UNITS):
             first = u * UNIT_TILES
             if u < SMALL_STORE_UNITS:
-                stores[first + 1] = [(first, 2)]
+                stores[first] = [(first, 1)]
+                stores[first + 1] = [(first + 1, 1)]
                 stores[first + 2] = [(first + 2, 2)]
             elif u < UNITS - 1:
                 stores[first + 2] = [(first, UNIT_TILES)]
             else:
                 stores[first + 1] = [(first, 2), (first + 3, 1)]
                 stores[first + 2] = [(first + 2, 1)]
-        late_sums = {(3 * n) // 2 + 1: (6 + n) * UNIT_TILES + SORTED_TILES for n in range(UNITS - 6)}
         unsummed = [
             u * UNIT_TILES + j for u in range(UNITS - LATE_UNITS, UNITS) for j in range(SORTED_TILES)
         ]
-        vector_sums = {3 + n: t for n, t in enumerate(unsummed)}
-        for t in range(TILES):
+        vector_sums = {5 + n: t for n, t in enumerate(unsummed)}
+        for n, t in enumerate(order):
             u, j = divmod(t, UNIT_TILES)
-            if t + LOOKAHEAD < TILES:
-                transpose_back(t + LOOKAHEAD)
-            if j == 0 and u < 2:
+            if n + LOOKAHEAD < TILES:
+                transpose_back(order[n + LOOKAHEAD])
+            if u not in results and u < 2:
                 results[u] = work.tile([P, UNIT_TILES, OUTS], F32, name="result", tag="grouped", align_bytes=64)
-            elif j == 0:
+            elif u not in results:
                 results[u] = keep.tile([P, UNIT_TILES, OUTS], F32, name="result", tag="unit_f32")
-            if j == 0:
-                if u in late_sums:
-                    sum_late(late_sums[u], "scalar")
-                finish_by_scalar_and_gpsimd(t + UNIT_TILES - 1)
-            if j < UNIT_TILES - 1:
+            if t in by_gpsimd:
+                if u > 4:
+                    sum_late(t, "scalar")
+                finish_by_scalar_and_gpsimd(t)
+            else:
                 finish_by_vector(t)
             if j == UNIT_TILES - 2 and u in vector_sums:
                 sum_late(vector_sums[u], "vector")
-            for first, n in stores.get(t, []):
-                store(first, n)
-            if t == 1:
+            for first, count in stores.get(t, []):
+                store(first, count)
+            if n == 2:
                 m_all = const.tile([P, OUTS], F32)
-                split = (OUT_CHUNKS - 1) * P
-                nc.scalar.copy(out=m_all[:, 0:split], in_=m_first[:, 0:split])
-                nc.scalar.copy(out=m_all[:, split:OUTS], in_=m_last[:, split:OUTS])
+                for half in range(2):
+                    nc.scalar.copy(
+                        out=m_all[:, half * OUTS // 2 : (half + 1) * OUTS // 2], in_=halves[half][:]
+                    )
                 nc.sync.dma_start(out=out_1.rearrange("(a o) -> a o", a=1), in_=m_all[0:1, :])

@@ -22,6 +22,8 @@ TILES = ROWS // P
 UNIT_TILES = 4
 UNIT_ROWS = UNIT_TILES * P
 UNITS = TILES // UNIT_TILES
+DUM = {(0, 1): 2, (1, 1): 1, (1, 2): 1}
+BY_TILE = 2
 LATE_UNITS = 3
 SORTED_TILES = 3
 SMALL_STORE_UNITS = 2
@@ -44,11 +46,13 @@ def tile_optimalnet_pb_t_kernel(tc, vi, W_words, W_scales, b, out_0, out_1):
         held_pool = stack.enter_context(tc.tile_pool(name="held", bufs=UNITS))
         raw_pool = stack.enter_context(tc.tile_pool(name="raw", bufs=3))
         work = stack.enter_context(tc.tile_pool(name="work", bufs=2))
+        sorted_pool = stack.enter_context(tc.tile_pool(name="sorted", bufs=1))
         psum = stack.enter_context(tc.psum_pool(name="psum", bufs=4))
         stack.enter_context(tc.manual_schedule())
 
         x_raw = {}
         held = {}
+        held_sorted = {}
         x_sorted = {}
         grouped = {}
         codes = {}
@@ -62,6 +66,15 @@ def tile_optimalnet_pb_t_kernel(tc, vi, W_words, W_scales, b, out_0, out_1):
             nc.sync.dma_start(out=held[u][:], in_=vi_tiles[:, u * UNIT_TILES + SORTED_TILES, :])
 
         load(0)
+        warm = const.tile([P, UNIT_ROWS], BF16)
+        nc.vector.memset(warm[:].bitcast(I32), 0)
+
+        def keep_warm(n):
+            bank = psum.tile([P, UNIT_ROWS], F32, name="warm_ps", tag="acc")
+            for m in range(n):
+                nc.tensor.matmul(bank[:], lhsT=warm[:, 0:P], rhs=warm[:], start=True, stop=True)
+
+        keep_warm(4)
 
         b_rows = const.tile([P, P], BF16)
         nc.vector.memset(b_rows[:], 0.0)
@@ -103,9 +116,17 @@ def tile_optimalnet_pb_t_kernel(tc, vi, W_words, W_scales, b, out_0, out_1):
             nc.tensor.transpose(b_ps[:, 0:P], b_rows_f32[:], ident[:])
             nc.scalar.copy(out=b_col[:], in_=b_ps[:, 0:OUT_CHUNKS])
 
+        scrap = const.tile([P, K], BF16)
+
+        def sum_first_tile():
+            nc.vector.tensor_scalar(
+                out=scrap[:], in0=x_raw[0][:, 0, :], scalar1=1.0, scalar2=None,
+                op0=ALU.mult, op1=ALU.add, accum_out=row_sum[:, 0:1],
+            )
+
         def sort_and_sum(u):
             x_sorted[u] = work.tile([P, SORTED_TILES, K], BF16, name="x_sorted")
-            for j in range(SORTED_TILES):
+            for j in range(u == 0, SORTED_TILES):
                 t = u * UNIT_TILES + j
                 if u >= UNITS - LATE_UNITS:
                     nc.vector.tensor_copy(
@@ -122,6 +143,13 @@ def tile_optimalnet_pb_t_kernel(tc, vi, W_words, W_scales, b, out_0, out_1):
                     op1=ALU.add,
                     accum_out=row_sum[:, t : t + 1],
                 )
+
+        def sort_late_held(u):
+            held_sorted[u] = sorted_pool.tile([P, K], BF16, name="held_sorted")
+            nc.vector.tensor_copy(
+                out=held_sorted[u][:].bitcast(F32).rearrange("p (h q) -> p h q", h=2),
+                in_=held[u][:].bitcast(F32).rearrange("p (q h) -> p h q", h=2),
+            )
 
         def sum_late(t, engine):
             u, j = divmod(t, UNIT_TILES)
@@ -141,6 +169,25 @@ def tile_optimalnet_pb_t_kernel(tc, vi, W_words, W_scales, b, out_0, out_1):
 
         def transpose_in(u):
             grouped[u] = work.tile([P, PASSES, UNIT_ROWS * PACK], BF16, name="grouped", tag="grouped", align_bytes=64)
+            if u < BY_TILE:
+                for j in range(UNIT_TILES):
+                    if DUM.get((u, j)):
+                        keep_warm(DUM[u, j])
+                    xt = psum.tile([P, PASSES, 2, P], F32, name="xt", tag="xt")
+                    for g in range(PASSES):
+                        for h in range(2):
+                            if (u, j) != (0, 0) and j < SORTED_TILES:
+                                first = h * (WORDS // 2) + g * P
+                                block = x_sorted[u][:, j, :].bitcast(F32)[:, first : first + P]
+                            else:
+                                rows = x_raw[u][:, j, :] if j < SORTED_TILES else held[u][:]
+                                block = rows.bitcast(F32)[:, 2 * P * g + h : 2 * P * (g + 1) : 2]
+                            nc.tensor.transpose(xt[:, g, h, :], block, ident[:])
+                    nc.scalar.copy(
+                        out=grouped[u][:].bitcast(F32).rearrange("p g (j r h) -> p j g r h", j=UNIT_TILES, h=2)[:, j],
+                        in_=xt[:].rearrange("p g h r -> p g r h"),
+                    )
+                return
             for g in range(PASSES):
                 words_g = grouped[u][:, g, :].bitcast(F32).rearrange("p (r h) -> p r h", h=2)
                 for half in range(2):
@@ -148,9 +195,10 @@ def tile_optimalnet_pb_t_kernel(tc, vi, W_words, W_scales, b, out_0, out_1):
                     for jj in range(2):
                         j = 2 * half + jj
                         for h in range(2):
-                            if j < SORTED_TILES:
+                            if j < SORTED_TILES or u >= UNITS - LATE_UNITS:
                                 first = h * (WORDS // 2) + g * P
-                                block = x_sorted[u][:, j, :].bitcast(F32)[:, first : first + P]
+                                rows = x_sorted[u][:, j, :] if j < SORTED_TILES else held_sorted[u][:]
+                                block = rows.bitcast(F32)[:, first : first + P]
                             else:
                                 block = held[u][:].bitcast(F32)[:, 2 * P * g + h : 2 * P * (g + 1) : 2]
                             nc.tensor.transpose(xt[:, h, jj * P : (jj + 1) * P], block, ident[:])
@@ -159,9 +207,13 @@ def tile_optimalnet_pb_t_kernel(tc, vi, W_words, W_scales, b, out_0, out_1):
                         in_=xt[:].rearrange("p h r -> p r h"),
                     )
 
-        def quantise(u):
-            words = work.tile([P, PASSES, UNIT_ROWS], U32, name="x_codes", align_bytes=64)
-            scales = work.tile([P, PASSES, UNIT_ROWS], U8, name="x_scales", align_bytes=64)
+        def quantise(u, only_pass=None):
+            if u not in codes:
+                codes[u] = (
+                    work.tile([P, PASSES, UNIT_ROWS], U32, name="x_codes", align_bytes=64),
+                    work.tile([P, PASSES, UNIT_ROWS], U8, name="x_scales", align_bytes=64),
+                )
+            words, scales = codes[u]
             if u < UNITS - 1:
                 nc.vector.quantize_mx(
                     out=words[:].rearrange("p g r -> p (g r)").bitcast(FP8X4),
@@ -169,11 +221,16 @@ def tile_optimalnet_pb_t_kernel(tc, vi, W_words, W_scales, b, out_0, out_1):
                     in_=grouped[u][:].rearrange("p g c -> p (g c)"),
                 )
             else:
-                for g in range(PASSES):
-                    nc.vector.quantize_mx(
-                        out=words[:, g, :].bitcast(FP8X4), scales=scales[:, g, :], in_=grouped[u][:, g, :]
-                    )
-            codes[u] = (words, scales)
+                g = only_pass
+                nc.vector.quantize_mx(
+                    out=words[:, g, :].bitcast(FP8X4), scales=scales[:, g, :], in_=grouped[u][:, g, :]
+                )
+
+        acc_banks = {}
+        later = set((u, 2) for u in range(UNITS - 1) if u >= UNITS - 3)
+
+        def by_vector(u, c):
+            return c == 0 or (u, c) in later or (c == 2 and u == UNITS - 1)
 
         def multiply(u):
             words, scales = codes[u]
@@ -193,6 +250,8 @@ def tile_optimalnet_pb_t_kernel(tc, vi, W_words, W_scales, b, out_0, out_1):
                 nc.vector.tensor_scalar(
                     out=partial[:], in0=partial[:], scalar1=1.0 / ROWS, scalar2=None, op0=ALU.mult
                 )
+            for c in range(OUT_CHUNKS):
+                acc_banks[u, c] = acc[c]
             for c, g in steps:
                 nc.tensor.matmul_mx(
                     out=acc[c][:],
@@ -203,47 +262,54 @@ def tile_optimalnet_pb_t_kernel(tc, vi, W_words, W_scales, b, out_0, out_1):
                     start=(g == 0),
                     stop=(g == PASSES - 1),
                 )
-                if g == PASSES - 1 and (c == 0 or (c == 2 and u == UNITS - 1)):
-                    nc.vector.scalar_tensor_tensor(
-                        out=vj_t[u][:, c, :],
-                        in0=acc[c][:],
-                        scalar=b_col[:, c : c + 1],
-                        in1=zeros[:],
-                        op0=ALU.add,
-                        op1=ALU.max,
-                        accum_out=col_sum[:, c, u : u + 1],
-                    )
-                    if u == UNITS - 1:
-                        nc.vector.tensor_scalar(
-                            out=repeated[:, c, :],
-                            in0=col_sum[:, c, u : u + 1].to_broadcast([P, P]),
-                            scalar1=1.0 / ROWS,
-                            scalar2=partial[:, c : c + 1],
-                            op0=ALU.mult,
-                            op1=ALU.add,
-                        )
-                elif g == PASSES - 1:
-                    nc.scalar.activation(
-                        out=vj_t[u][:, c, :],
-                        in_=acc[c][:],
-                        func=ACT.Relu,
-                        bias=b_col[:, c : c + 1],
-                        scale=1.0,
-                        accum_out=col_sum[:, c, u : u + 1],
-                    )
-                    if u == UNITS - 1:
-                        nc.scalar.activation(
-                            out=repeated[:, c, :],
-                            in_=col_sum[:, c, u : u + 1].to_broadcast([P, P]),
-                            func=ACT.Identity,
-                            bias=partial[:, c : c + 1],
-                            scale=1.0 / ROWS,
-                        )
+                if g == PASSES - 1 and u == UNITS - 2 and c == 0:
+                    quantise(u + 1, 0)
+                if g == PASSES - 1 and (u, c) not in later:
+                    empty_bank(u, c)
 
-        nc.scalar.copy(out=b_rows_f32[:], in_=b_rows[:])
+        def empty_bank(u, c):
+            bank = acc_banks[u, c]
+            if by_vector(u, c):
+                nc.vector.scalar_tensor_tensor(
+                    out=vj_t[u][:, c, :],
+                    in0=bank[:],
+                    scalar=b_col[:, c : c + 1],
+                    in1=zeros[:],
+                    op0=ALU.add,
+                    op1=ALU.max,
+                    accum_out=col_sum[:, c, u : u + 1],
+                )
+                if u == UNITS - 1:
+                    nc.vector.tensor_scalar(
+                        out=repeated[:, c, :],
+                        in0=col_sum[:, c, u : u + 1].to_broadcast([P, P]),
+                        scalar1=1.0 / ROWS,
+                        scalar2=partial[:, c : c + 1],
+                        op0=ALU.mult,
+                        op1=ALU.add,
+                    )
+            else:
+                nc.scalar.activation(
+                    out=vj_t[u][:, c, :],
+                    in_=bank[:],
+                    func=ACT.Relu,
+                    bias=b_col[:, c : c + 1],
+                    scale=1.0,
+                    accum_out=col_sum[:, c, u : u + 1],
+                )
+                if u == UNITS - 1:
+                    nc.scalar.activation(
+                        out=repeated[:, c, :],
+                        in_=col_sum[:, c, u : u + 1].to_broadcast([P, P]),
+                        func=ACT.Identity,
+                        bias=partial[:, c : c + 1],
+                        scale=1.0 / ROWS,
+                    )
+
+        sum_first_tile()
         sort_and_sum(0)
         transpose_in(0)
-        bias_to_partitions()
+        nc.scalar.copy(out=b_rows_f32[:], in_=b_rows[:])
         sort_and_sum(1)
         quantise(0)
         for i in range(UNITS):
@@ -251,17 +317,21 @@ def tile_optimalnet_pb_t_kernel(tc, vi, W_words, W_scales, b, out_0, out_1):
                 load(i + 3)
             if i + 2 < UNITS:
                 sort_and_sum(i + 2)
+                if i + 2 >= UNITS - LATE_UNITS:
+                    sort_late_held(i + 2)
             if i + 1 < UNITS:
                 transpose_in(i + 1)
-            if i == UNITS - 2:
-                sum_late(3, "vector")
-                sum_late(7, "vector")
-                sum_late(11, "vector")
+            if i == 0:
+                bias_to_partitions()
+            if i >= UNITS - 4 and i < UNITS - 1:
+                sum_late((i - UNITS + 4) * UNIT_TILES + SORTED_TILES, "vector")
             if i == UNITS - 1:
                 sum_late(15, "scalar")
             multiply(i)
             if i + 1 < UNITS:
-                quantise(i + 1)
+                quantise(i + 1, 1)
+            if (i, 2) in later:
+                empty_bank(i, 2)
 
         banks = {}
         results = {}

@@ -23,6 +23,8 @@ UNIT_TILES = 4
 UNIT_ROWS = UNIT_TILES * P
 UNITS = TILES // UNIT_TILES
 DUM = {(0, 1): 2, (1, 1): 1, (1, 2): 1}
+EARLY = 2
+HALVES = 4
 BY_TILE = 2
 LATE_UNITS = 3
 SORTED_TILES = 3
@@ -227,7 +229,7 @@ def tile_optimalnet_pb_t_kernel(tc, vi, W_words, W_scales, b, out_0, out_1):
                 )
 
         acc_banks = {}
-        later = set((u, 2) for u in range(UNITS - 1) if u >= UNITS - 3)
+        later = set((u, 2) for u in range(UNITS - 1) if u >= UNITS - 3 or u % 4 == 2)
 
         def by_vector(u, c):
             return c == 0 or (u, c) in later or (c == 2 and u == UNITS - 1)
@@ -348,13 +350,13 @@ def tile_optimalnet_pb_t_kernel(tc, vi, W_words, W_scales, b, out_0, out_1):
                 else:
                     nc.tensor.transpose(banks[t][:, c * P : (c + 1) * P], block, ident[:])
 
-        def finish_by_vector(t):
+        def finish_by_vector(t, cols=slice(0, OUTS)):
             u, j = divmod(t, UNIT_TILES)
             nc.vector.scalar_tensor_tensor(
-                out=results[u][:, j, :],
-                in0=mc_all[:],
+                out=results[u][:, j, cols],
+                in0=mc_all[:, cols],
                 scalar=row_sum[:, t : t + 1],
-                in1=banks[t][:],
+                in1=banks[t][:, cols],
                 op0=ALU.mult,
                 op1=ALU.add,
             )
@@ -370,9 +372,11 @@ def tile_optimalnet_pb_t_kernel(tc, vi, W_words, W_scales, b, out_0, out_1):
                 out=results[u][:, j, :], in0=results[u][:, j, :], in1=correction[:], op=ALU.add
             )
 
-        def store(first, n):
+        def store(first, n, cols=slice(0, OUTS)):
             u, j = divmod(first, UNIT_TILES)
-            nc.sync.dma_start(out=out_tiles[:, first : first + n, :], in_=results[u][:, j : j + n, :])
+            nc.sync.dma_start(
+                out=out_tiles[:, first : first + n, cols], in_=results[u][:, j : j + n, cols]
+            )
 
         mc_all = const.tile([P, OUTS], F32)
         order = list(range(UNIT_TILES))
@@ -390,19 +394,22 @@ def tile_optimalnet_pb_t_kernel(tc, vi, W_words, W_scales, b, out_0, out_1):
             halves.append(m_ps)
             if half == 0:
                 transpose_back(order[1])
-        nc.scalar.mul(out=mc_all[:, 0 : OUTS // 2], in_=halves[0][:], mul=C)
         nc.vector.tensor_scalar(
-            out=mc_all[:, OUTS // 2 : OUTS], in0=halves[1][:], scalar1=C, scalar2=None, op0=ALU.mult
+            out=mc_all[:, 0 : OUTS // 2], in0=halves[0][:], scalar1=C, scalar2=None, op0=ALU.mult
         )
+        nc.scalar.mul(out=mc_all[:, OUTS // 2 : OUTS], in_=halves[1][:], mul=C)
         for t in order[2:LOOKAHEAD]:
             transpose_back(t)
 
-        stores = {0: [(0, 1)], 1: [(1, 1)], 2: [(2, 1)], 3: [(3, 1)]}
+        stores = {2: [(2, 1)], 3: [(3, 1)]}
         for u in range(1, UNITS):
             first = u * UNIT_TILES
             if u < SMALL_STORE_UNITS:
                 stores[first] = [(first, 1)]
                 stores[first + 1] = [(first + 1, 1)]
+                stores[first + 2] = [(first + 2, 2)]
+            elif u < HALVES:
+                stores[first + 1] = [(first, 2)]
                 stores[first + 2] = [(first + 2, 2)]
             elif u < UNITS - 1:
                 stores[first + 2] = [(first, UNIT_TILES)]
@@ -425,7 +432,13 @@ def tile_optimalnet_pb_t_kernel(tc, vi, W_words, W_scales, b, out_0, out_1):
                 if u > 4:
                     sum_late(t, "scalar")
                 finish_by_scalar_and_gpsimd(t)
-            else:
+            elif n == 0:
+                for half in range(2):
+                    cols = slice(half * OUTS // 2, (half + 1) * OUTS // 2)
+                    for first in range(EARLY):
+                        finish_by_vector(first, cols)
+                        store(first, 1, cols)
+            elif n >= EARLY:
                 finish_by_vector(t)
             if j == UNIT_TILES - 2 and u in vector_sums:
                 sum_late(vector_sums[u], "vector")
@@ -437,4 +450,5 @@ def tile_optimalnet_pb_t_kernel(tc, vi, W_words, W_scales, b, out_0, out_1):
                     nc.scalar.copy(
                         out=m_all[:, half * OUTS // 2 : (half + 1) * OUTS // 2], in_=halves[half][:]
                     )
+            if n == 12:
                 nc.sync.dma_start(out=out_1.rearrange("(a o) -> a o", a=1), in_=m_all[0:1, :])

@@ -49,6 +49,7 @@ def tile_optimalnet_pb_t_kernel(tc, vi, W_words, W_scales, b, out_0, out_1):
         raw_pool = stack.enter_context(tc.tile_pool(name="raw", bufs=3))
         work = stack.enter_context(tc.tile_pool(name="work", bufs=2))
         sorted_pool = stack.enter_context(tc.tile_pool(name="sorted", bufs=1))
+        extra_pool = stack.enter_context(tc.tile_pool(name="extra", bufs=3))
         psum = stack.enter_context(tc.psum_pool(name="psum", bufs=4))
         stack.enter_context(tc.manual_schedule())
 
@@ -60,15 +61,24 @@ def tile_optimalnet_pb_t_kernel(tc, vi, W_words, W_scales, b, out_0, out_1):
         codes = {}
         vj_t = {}
 
+        put_off = [(5, 2), (8, 2), (11, 2)]
+        extra = {}
+
+        def raw_tile(u, j):
+            if (u, j) in put_off:
+                return extra[u, j][:]
+            return x_raw[u][:, j, :] if j < SORTED_TILES else held[u][:]
+
         def load(u):
             x_raw[u] = raw_pool.tile([P, SORTED_TILES, K], BF16, name="x_raw")
             held[u] = held_pool.tile([P, K], BF16, name="held")
-            for j in range(SORTED_TILES):
-                nc.sync.dma_start(out=x_raw[u][:, j, :], in_=vi_tiles[:, u * UNIT_TILES + j, :])
-            nc.sync.dma_start(out=held[u][:], in_=vi_tiles[:, u * UNIT_TILES + SORTED_TILES, :])
+            for j in range(UNIT_TILES):
+                if (u, j) in put_off:
+                    extra[u, j] = extra_pool.tile([P, K], BF16, name="extra")
+                nc.sync.dma_start(out=raw_tile(u, j), in_=vi_tiles[:, u * UNIT_TILES + j, :])
 
         load(0)
-        warm = const.tile([P, UNIT_ROWS], BF16)
+        warm = work.tile([P, UNIT_ROWS], BF16, name="warm", tag="correction")
         nc.vector.memset(warm[:].bitcast(I32), 0)
 
         def keep_warm(n):
@@ -118,7 +128,7 @@ def tile_optimalnet_pb_t_kernel(tc, vi, W_words, W_scales, b, out_0, out_1):
             nc.tensor.transpose(b_ps[:, 0:P], b_rows_f32[:], ident[:])
             nc.scalar.copy(out=b_col[:], in_=b_ps[:, 0:OUT_CHUNKS])
 
-        scrap = const.tile([P, K], BF16)
+        scrap = work.tile([P, K], BF16, name="scrap", tag="correction")
 
         def sum_first_tile():
             nc.vector.tensor_scalar(
@@ -130,6 +140,8 @@ def tile_optimalnet_pb_t_kernel(tc, vi, W_words, W_scales, b, out_0, out_1):
             x_sorted[u] = work.tile([P, SORTED_TILES, K], BF16, name="x_sorted")
             for j in range(u == 0, SORTED_TILES):
                 t = u * UNIT_TILES + j
+                if (u, j) in put_off:
+                    continue
                 if u >= UNITS - LATE_UNITS:
                     nc.vector.tensor_copy(
                         out=x_sorted[u][:, j, :].bitcast(F32).rearrange("p (h q) -> p h q", h=2),
@@ -155,7 +167,7 @@ def tile_optimalnet_pb_t_kernel(tc, vi, W_words, W_scales, b, out_0, out_1):
 
         def sum_late(t, engine):
             u, j = divmod(t, UNIT_TILES)
-            rows = x_raw[u][:, j, :] if j < SORTED_TILES else held[u][:]
+            rows = raw_tile(u, j)
             if engine == "vector":
                 nc.vector.tensor_scalar(
                     out=rows,
@@ -168,6 +180,27 @@ def tile_optimalnet_pb_t_kernel(tc, vi, W_words, W_scales, b, out_0, out_1):
                 )
             else:
                 nc.scalar.activation(out=rows, in_=rows, func=ACT.Copy, accum_out=row_sum[:, t : t + 1])
+
+        folded = {}
+
+        def fold_on_gpsimd(t, fold):
+            rows = raw_tile(*divmod(t, UNIT_TILES))
+            nc.gpsimd.tensor_tensor(
+                out=fold[:, 0 : K // 2], in0=rows[:, 0 : K // 2], in1=rows[:, K // 2 : K], op=ALU.add
+            )
+            width = K // 4
+            while width >= 64:
+                nc.gpsimd.tensor_tensor(
+                    out=fold[:, 0:width], in0=fold[:, 0:width], in1=fold[:, width : 2 * width], op=ALU.add
+                )
+                width //= 2
+            folded[t] = fold
+
+        def sum_folded(t):
+            nc.scalar.activation(
+                out=folded[t][:, 0:64], in_=folded[t][:, 0:64], func=ACT.Copy,
+                accum_out=row_sum[:, t : t + 1],
+            )
 
         def transpose_in(u):
             grouped[u] = work.tile([P, PASSES, UNIT_ROWS * PACK], BF16, name="grouped", tag="grouped", align_bytes=64)
@@ -197,12 +230,12 @@ def tile_optimalnet_pb_t_kernel(tc, vi, W_words, W_scales, b, out_0, out_1):
                     for jj in range(2):
                         j = 2 * half + jj
                         for h in range(2):
-                            if j < SORTED_TILES or u >= UNITS - LATE_UNITS:
+                            if (u, j) not in put_off and (j < SORTED_TILES or u >= UNITS - LATE_UNITS):
                                 first = h * (WORDS // 2) + g * P
                                 rows = x_sorted[u][:, j, :] if j < SORTED_TILES else held_sorted[u][:]
                                 block = rows.bitcast(F32)[:, first : first + P]
                             else:
-                                block = held[u][:].bitcast(F32)[:, 2 * P * g + h : 2 * P * (g + 1) : 2]
+                                block = raw_tile(u, j).bitcast(F32)[:, 2 * P * g + h : 2 * P * (g + 1) : 2]
                             nc.tensor.transpose(xt[:, h, jj * P : (jj + 1) * P], block, ident[:])
                     nc.scalar.copy(
                         out=words_g[:, half * 2 * P : (half + 1) * 2 * P, :],
@@ -229,7 +262,7 @@ def tile_optimalnet_pb_t_kernel(tc, vi, W_words, W_scales, b, out_0, out_1):
                 )
 
         acc_banks = {}
-        later = set((u, 2) for u in range(UNITS - 1) if u >= UNITS - 3 or u % 4 == 2)
+        later = set((u, 2) for u in range(UNITS - 1) if u >= UNITS - 3 or u in (5, 10))
 
         def by_vector(u, c):
             return c == 0 or (u, c) in later or (c == 2 and u == UNITS - 1)
@@ -245,7 +278,7 @@ def tile_optimalnet_pb_t_kernel(tc, vi, W_words, W_scales, b, out_0, out_1):
             else:
                 steps = [(c, g) for g in range(PASSES) for c in range(OUT_CHUNKS)]
             if u == UNITS - 1:
-                sum_late(19, "vector")
+                sum_late(23, "vector")
                 nc.vector.tensor_reduce(
                     out=partial[:], in_=col_sum[:, :, 0:u], axis=mybir.AxisListType.X, op=ALU.add
                 )
@@ -313,6 +346,7 @@ def tile_optimalnet_pb_t_kernel(tc, vi, W_words, W_scales, b, out_0, out_1):
         transpose_in(0)
         nc.scalar.copy(out=b_rows_f32[:], in_=b_rows[:])
         sort_and_sum(1)
+        fold_on_gpsimd(3, work.tile([P, K // 2], F32, name="fold", tag="correction"))
         quantise(0)
         for i in range(UNITS):
             if i + 3 < UNITS:
@@ -326,9 +360,10 @@ def tile_optimalnet_pb_t_kernel(tc, vi, W_words, W_scales, b, out_0, out_1):
             if i == 0:
                 bias_to_partitions()
             if i >= UNITS - 4 and i < UNITS - 1:
-                sum_late((i - UNITS + 4) * UNIT_TILES + SORTED_TILES, "vector")
+                sum_late((i - UNITS + 5) * UNIT_TILES + SORTED_TILES, "vector")
             if i == UNITS - 1:
-                sum_late(15, "scalar")
+                sum_late(19, "scalar")
+                sum_folded(3)
             multiply(i)
             if i + 1 < UNITS:
                 quantise(i + 1, 1)
@@ -364,9 +399,19 @@ def tile_optimalnet_pb_t_kernel(tc, vi, W_words, W_scales, b, out_0, out_1):
         def finish_by_scalar_and_gpsimd(t):
             u, j = divmod(t, UNIT_TILES)
             correction = work.tile([P, OUTS], F32, name="correction")
-            nc.scalar.activation(
-                out=correction[:], in_=mc_all[:], func=ACT.Copy, scale=row_sum[:, t : t + 1]
-            )
+            if u in (3, 5, 7, 9, 11, 13):
+                nc.gpsimd.tensor_scalar(
+                    out=correction[:],
+                    in0=mc_all[:],
+                    scalar1=row_sum[:, t : t + 1],
+                    scalar2=0.0,
+                    op0=ALU.mult,
+                    op1=ALU.add,
+                )
+            else:
+                nc.scalar.activation(
+                    out=correction[:], in_=mc_all[:], func=ACT.Copy, scale=row_sum[:, t : t + 1]
+                )
             nc.scalar.copy(out=results[u][:, j, :], in_=banks[t][:])
             nc.gpsimd.tensor_tensor(
                 out=results[u][:, j, :], in0=results[u][:, j, :], in1=correction[:], op=ALU.add
@@ -429,7 +474,9 @@ def tile_optimalnet_pb_t_kernel(tc, vi, W_words, W_scales, b, out_0, out_1):
             elif u not in results:
                 results[u] = keep.tile([P, UNIT_TILES, OUTS], F32, name="result", tag="unit_f32")
             if t in by_gpsimd:
-                if u > 4:
+                if u in {3: 22, 5: 34, 7: 46}:
+                    sum_late({3: 22, 5: 34, 7: 46}[u], "scalar")
+                if u > 5:
                     sum_late(t, "scalar")
                 finish_by_scalar_and_gpsimd(t)
             elif n == 0:
@@ -445,7 +492,7 @@ def tile_optimalnet_pb_t_kernel(tc, vi, W_words, W_scales, b, out_0, out_1):
             for first, count in stores.get(t, []):
                 store(first, count)
             if n == 2:
-                m_all = const.tile([P, OUTS], F32)
+                m_all = work.tile([P, OUTS], F32, name="m_all", tag="x_sorted")
                 for half in range(2):
                     nc.scalar.copy(
                         out=m_all[:, half * OUTS // 2 : (half + 1) * OUTS // 2], in_=halves[half][:]

@@ -45,11 +45,11 @@ def tile_optimalnet_pb_t_kernel(tc, vi, W_words, W_scales, b, out_0, out_1):
     with ExitStack() as stack:
         const = stack.enter_context(tc.tile_pool(name="const", bufs=1))
         keep = stack.enter_context(tc.tile_pool(name="keep", bufs=UNITS))
-        held_pool = stack.enter_context(tc.tile_pool(name="held", bufs=UNITS))
+        held_pool = stack.enter_context(tc.tile_pool(name="held", bufs=UNITS - 1))
         raw_pool = stack.enter_context(tc.tile_pool(name="raw", bufs=3))
         work = stack.enter_context(tc.tile_pool(name="work", bufs=2))
         sorted_pool = stack.enter_context(tc.tile_pool(name="sorted", bufs=1))
-        extra_pool = stack.enter_context(tc.tile_pool(name="extra", bufs=3))
+        extra_pool = stack.enter_context(tc.tile_pool(name="extra", bufs=4))
         psum = stack.enter_context(tc.psum_pool(name="psum", bufs=4))
         stack.enter_context(tc.manual_schedule())
 
@@ -61,7 +61,7 @@ def tile_optimalnet_pb_t_kernel(tc, vi, W_words, W_scales, b, out_0, out_1):
         codes = {}
         vj_t = {}
 
-        put_off = [(5, 2), (8, 2), (11, 2)]
+        put_off = [(4, 2), (7, 2), (10, 2), (12, 2)]
         extra = {}
 
         def raw_tile(u, j):
@@ -158,6 +158,17 @@ def tile_optimalnet_pb_t_kernel(tc, vi, W_words, W_scales, b, out_0, out_1):
                     accum_out=row_sum[:, t : t + 1],
                 )
 
+        def sort_held_on_gpsimd(u):
+            held_sorted[u] = sorted_pool.tile([P, K], BF16, name="held_sorted")
+            nc.gpsimd.tensor_scalar(
+                out=held_sorted[u][:].rearrange("p (h q e) -> p h q e", h=2, e=2),
+                in0=held[u][:].rearrange("p (q h e) -> p h q e", h=2, e=2),
+                scalar1=1.0,
+                scalar2=0.0,
+                op0=ALU.mult,
+                op1=ALU.add,
+            )
+
         def sort_late_held(u):
             held_sorted[u] = sorted_pool.tile([P, K], BF16, name="held_sorted")
             nc.vector.tensor_copy(
@@ -230,7 +241,7 @@ def tile_optimalnet_pb_t_kernel(tc, vi, W_words, W_scales, b, out_0, out_1):
                     for jj in range(2):
                         j = 2 * half + jj
                         for h in range(2):
-                            if (u, j) not in put_off and (j < SORTED_TILES or u >= UNITS - LATE_UNITS):
+                            if (u, j) not in put_off and (j < SORTED_TILES or u in held_sorted):
                                 first = h * (WORDS // 2) + g * P
                                 rows = x_sorted[u][:, j, :] if j < SORTED_TILES else held_sorted[u][:]
                                 block = rows.bitcast(F32)[:, first : first + P]
@@ -355,6 +366,8 @@ def tile_optimalnet_pb_t_kernel(tc, vi, W_words, W_scales, b, out_0, out_1):
                 sort_and_sum(i + 2)
                 if i + 2 >= UNITS - LATE_UNITS:
                     sort_late_held(i + 2)
+                elif True:
+                    sort_held_on_gpsimd(i + 2)
             if i + 1 < UNITS:
                 transpose_in(i + 1)
             if i == 0:
@@ -474,8 +487,8 @@ def tile_optimalnet_pb_t_kernel(tc, vi, W_words, W_scales, b, out_0, out_1):
             elif u not in results:
                 results[u] = keep.tile([P, UNIT_TILES, OUTS], F32, name="result", tag="unit_f32")
             if t in by_gpsimd:
-                if u in {3: 22, 5: 34, 7: 46}:
-                    sum_late({3: 22, 5: 34, 7: 46}[u], "scalar")
+                if u in {3: 18, 5: 30, 7: 42, 9: 50}:
+                    sum_late({3: 18, 5: 30, 7: 42, 9: 50}[u], "scalar")
                 if u > 5:
                     sum_late(t, "scalar")
                 finish_by_scalar_and_gpsimd(t)

from contextlib import ExitStack

import concourse.mybir as mybir
from concourse.masks import make_identity

F32 = mybir.dt.float32
BF16 = mybir.dt.bfloat16
I32 = mybir.dt.int32
U32 = mybir.dt.uint32
U8 = mybir.dt.uint8
FP8X4 = mybir.dt.float8_e4m3fn_x4
FP4X4 = mybir.dt.float4_e2m1fn_x4
ALU = mybir.AluOpType
ACT = mybir.ActivationFunctionType

P = 128
ROWS, K, OUTS = 8192, 1024, 512
PACK = 4
K_PASS = P * PACK
PASSES = K // K_PASS
TILES = ROWS // P
UNIT_TILES = 4
UNIT_ROWS = UNIT_TILES * P
UNITS = TILES // UNIT_TILES
DUM = {(0, 1): 2, (1, 1): 1, (1, 2): 1}
EARLY = 2
HALVES = 4
BY_TILE = 2
LATE_UNITS = 3
SORTED_TILES = 3
SMALL_STORE_UNITS = 2
LOOKAHEAD = 6
OUT_CHUNKS = OUTS // P
WORDS = K // 2
C = 0.01 * 0.001 / 1

FLOPS = 2 * ROWS * K * OUTS


def tile_optimalnet_pb_t_kernel(tc, vi, W_words, W_scales, b, out_0, out_1):
    nc = tc.nc
    vi_tiles = vi.rearrange("(p t) k -> p t k", t=TILES)
    out_tiles = out_0.rearrange("(p t) o -> p t o", t=TILES)

    with ExitStack() as stack:
        const = stack.enter_context(tc.tile_pool(name="const", bufs=1))
        keep = stack.enter_context(tc.tile_pool(name="keep", bufs=UNITS))
        held_pool = stack.enter_context(tc.tile_pool(name="held", bufs=UNITS - 1))
        raw_pool = stack.enter_context(tc.tile_pool(name="raw", bufs=3))
        work = stack.enter_context(tc.tile_pool(name="work", bufs=2))
        sorted_pool = stack.enter_context(tc.tile_pool(name="sorted", bufs=1))
        extra_pool = stack.enter_context(tc.tile_pool(name="extra", bufs=4))
        psum = stack.enter_context(tc.psum_pool(name="psum", bufs=4))
        stack.enter_context(tc.manual_schedule())

        x_raw = {}
        held = {}
        held_sorted = {}
        x_sorted = {}
        grouped = {}
        codes = {}
        vj_t = {}

        put_off = [(4, 2), (7, 2), (10, 2), (12, 2)]
        extra = {}

        def raw_tile(u, j):
            if (u, j) in put_off:
                return extra[u, j][:]
            return x_raw[u][:, j, :] if j < SORTED_TILES else held[u][:]

        def load(u):
            x_raw[u] = raw_pool.tile([P, SORTED_TILES, K], BF16, name="x_raw")
            held[u] = held_pool.tile([P, K], BF16, name="held")
            for j in range(UNIT_TILES):
                if (u, j) in put_off:
                    extra[u, j] = extra_pool.tile([P, K], BF16, name="extra")
                nc.sync.dma_start(out=raw_tile(u, j), in_=vi_tiles[:, u * UNIT_TILES + j, :])

        load(0)
        warm = work.tile([P, UNIT_ROWS], BF16, name="warm", tag="correction")
        nc.vector.memset(warm[:].bitcast(I32), 0)

        def keep_warm(n):
            bank = psum.tile([P, UNIT_ROWS], F32, name="warm_ps", tag="acc")
            for m in range(n):
                nc.tensor.matmul(bank[:], lhsT=warm[:, 0:P], rhs=warm[:], start=True, stop=True)

        keep_warm(4)

        b_rows = const.tile([P, P], BF16)
        nc.vector.memset(b_rows[:], 0.0)
        nc.scalar.dma_start(out=b_rows[0:OUT_CHUNKS, :], in_=b.rearrange("(c o) -> c o", o=P))

        load(1)

        w_words = const.tile([P, PASSES, 2 * OUTS], U8, align_bytes=64)
        nc.sync.dma_start(
            out=w_words[:].bitcast(I32), in_=W_words.bitcast(I32).rearrange("g p w -> p g w")
        )
        w_scales = const.tile([P, PASSES, OUTS], U8, align_bytes=64)
        nc.vector.memset(w_scales[:].bitcast(I32), 0)
        for quad in range(4):
            nc.sync.dma_start(
                out=w_scales[32 * quad : 32 * quad + 4, :, :].bitcast(I32),
                in_=W_scales.bitcast(I32)[:, 4 * quad : 4 * quad + 4, :].rearrange(
                    "g r w -> r g w"
                ),
            )
        load(2)

        ident = const.tile([P, P], F32)
        make_identity(nc, ident[:])
        zeros = const.tile([P, UNIT_ROWS], F32)
        nc.vector.memset(zeros[:], 0.0)
        b_col = const.tile([P, OUT_CHUNKS], F32)

        row_sum = const.tile([P, TILES], F32)
        col_sum = const.tile([P, OUT_CHUNKS, UNITS], F32)

        partial = const.tile([P, OUT_CHUNKS], F32)
        repeated = const.tile([P, OUT_CHUNKS, P], F32)

        b_rows_f32 = const.tile([P, P], F32)

        def bias_to_partitions():
            b_ps = psum.tile([P, OUTS], F32, tag="acc")
            nc.tensor.transpose(b_ps[:, 0:P], b_rows_f32[:], ident[:])
            nc.scalar.copy(out=b_col[:], in_=b_ps[:, 0:OUT_CHUNKS])

        scrap = work.tile([P, K], BF16, name="scrap", tag="correction")

        def sum_first_tile():
            nc.vector.tensor_scalar(
                out=scrap[:], in0=x_raw[0][:, 0, :], scalar1=1.0, scalar2=None,
                op0=ALU.mult, op1=ALU.add, accum_out=row_sum[:, 0:1],
            )

        def sort_and_sum(u):
            x_sorted[u] = work.tile([P, SORTED_TILES, K], BF16, name="x_sorted")
            for j in range(u == 0, SORTED_TILES):
                t = u * UNIT_TILES + j
                if (u, j) in put_off:
                    continue
                if u >= UNITS - LATE_UNITS:
                    nc.vector.tensor_copy(
                        out=x_sorted[u][:, j, :].bitcast(F32).rearrange("p (h q) -> p h q", h=2),
                        in_=x_raw[u][:, j, :].bitcast(F32).rearrange("p (q h) -> p h q", h=2),
                    )
                    continue
                nc.vector.tensor_scalar(
                    out=x_sorted[u][:, j, :].rearrange("p (h q e) -> p h q e", h=2, e=2),
                    in0=x_raw[u][:, j, :].rearrange("p (q h e) -> p h q e", h=2, e=2),
                    scalar1=1.0,
                    scalar2=None,
                    op0=ALU.mult,
                    op1=ALU.add,
                    accum_out=row_sum[:, t : t + 1],
                )

        def sort_held_on_gpsimd(u):
            held_sorted[u] = sorted_pool.tile([P, K], BF16, name="held_sorted")
            nc.gpsimd.tensor_scalar(
                out=held_sorted[u][:].rearrange("p (h q e) -> p h q e", h=2, e=2),
                in0=held[u][:].rearrange("p (q h e) -> p h q e", h=2, e=2),
                scalar1=1.0,
                scalar2=0.0,
                op0=ALU.mult,
                op1=ALU.add,
            )

        def sort_late_held(u):
            held_sorted[u] = sorted_pool.tile([P, K], BF16, name="held_sorted")
            nc.vector.tensor_copy(
                out=held_sorted[u][:].bitcast(F32).rearrange("p (h q) -> p h q", h=2),
                in_=held[u][:].bitcast(F32).rearrange("p (q h) -> p h q", h=2),
            )

        def sum_late(t, engine):
            u, j = divmod(t, UNIT_TILES)
            rows = raw_tile(u, j)
            if engine == "vector":
                nc.vector.tensor_scalar(
                    out=rows,
                    in0=rows,
                    scalar1=1.0,
                    scalar2=None,
                    op0=ALU.mult,
                    op1=ALU.add,
                    accum_out=row_sum[:, t : t + 1],
                )
            else:
                nc.scalar.activation(out=rows, in_=rows, func=ACT.Copy, accum_out=row_sum[:, t : t + 1])

        folded = {}

        def fold_on_gpsimd(t, fold):
            rows = raw_tile(*divmod(t, UNIT_TILES))
            nc.gpsimd.tensor_tensor(
                out=fold[:, 0 : K // 2], in0=rows[:, 0 : K // 2], in1=rows[:, K // 2 : K], op=ALU.add
            )
            width = K // 4
            while width >= 64:
                nc.gpsimd.tensor_tensor(
                    out=fold[:, 0:width], in0=fold[:, 0:width], in1=fold[:, width : 2 * width], op=ALU.add
                )
                width //= 2
            folded[t] = fold

        def sum_folded(t):
            nc.scalar.activation(
                out=folded[t][:, 0:64], in_=folded[t][:, 0:64], func=ACT.Copy,
                accum_out=row_sum[:, t : t + 1],
            )

        def transpose_in(u):
            grouped[u] = work.tile([P, PASSES, UNIT_ROWS * PACK], BF16, name="grouped", tag="grouped", align_bytes=64)
            if u < BY_TILE:
                for j in range(UNIT_TILES):
                    if DUM.get((u, j)):
                        keep_warm(DUM[u, j])
                    xt = psum.tile([P, PASSES, 2, P], F32, name="xt", tag="xt")
                    for g in range(PASSES):
                        for h in range(2):
                            if (u, j) != (0, 0) and j < SORTED_TILES:
                                first = h * (WORDS // 2) + g * P
                                block = x_sorted[u][:, j, :].bitcast(F32)[:, first : first + P]
                            else:
                                rows = x_raw[u][:, j, :] if j < SORTED_TILES else held[u][:]
                                block = rows.bitcast(F32)[:, 2 * P * g + h : 2 * P * (g + 1) : 2]
                            nc.tensor.transpose(xt[:, g, h, :], block, ident[:])
                    nc.scalar.copy(
                        out=grouped[u][:].bitcast(F32).rearrange("p g (j r h) -> p j g r h", j=UNIT_TILES, h=2)[:, j],
                        in_=xt[:].rearrange("p g h r -> p g r h"),
                    )
                return
            for g in range(PASSES):
                words_g = grouped[u][:, g, :].bitcast(F32).rearrange("p (r h) -> p r h", h=2)
                for half in range(2):
                    xt = psum.tile([P, 2, 2 * P], F32, tag="xt")
                    for jj in range(2):
                        j = 2 * half + jj
                        for h in range(2):
                            if (u, j) not in put_off and (j < SORTED_TILES or u in held_sorted):
                                first = h * (WORDS // 2) + g * P
                                rows = x_sorted[u][:, j, :] if j < SORTED_TILES else held_sorted[u][:]
                                block = rows.bitcast(F32)[:, first : first + P]
                            else:
                                block = raw_tile(u, j).bitcast(F32)[:, 2 * P * g + h : 2 * P * (g + 1) : 2]
                            nc.tensor.transpose(xt[:, h, jj * P : (jj + 1) * P], block, ident[:])
                    nc.scalar.copy(
                        out=words_g[:, half * 2 * P : (half + 1) * 2 * P, :],
                        in_=xt[:].rearrange("p h r -> p r h"),
                    )

        def quantise(u, only_pass=None):
            if u not in codes:
                codes[u] = (
                    work.tile([P, PASSES, UNIT_ROWS], U32, name="x_codes", align_bytes=64),
                    work.tile([P, PASSES, UNIT_ROWS], U8, name="x_scales", align_bytes=64),
                )
            words, scales = codes[u]
            if u < UNITS - 1:
                nc.vector.quantize_mx(
                    out=words[:].rearrange("p g r -> p (g r)").bitcast(FP8X4),
                    scales=scales[:].rearrange("p g r -> p (g r)"),
                    in_=grouped[u][:].rearrange("p g c -> p (g c)"),
                )
            else:
                g = only_pass
                nc.vector.quantize_mx(
                    out=words[:, g, :].bitcast(FP8X4), scales=scales[:, g, :], in_=grouped[u][:, g, :]
                )

        acc_banks = {}
        later = set((u, 2) for u in range(UNITS - 1) if u >= UNITS - 3 or u in (5, 10))

        def by_vector(u, c):
            return c == 0 or (u, c) in later or (c == 2 and u == UNITS - 1)

        def multiply(u):
            words, scales = codes[u]
            vj_t[u] = keep.tile([P, OUT_CHUNKS, UNIT_ROWS], F32, name="vj_t", tag="unit_f32")
            acc = {}
            for c in range(OUT_CHUNKS):
                acc[c] = psum.tile([P, UNIT_ROWS], F32, name="acc", tag="acc")
            if u < UNITS - 1:
                steps = [(c, g) for c in range(OUT_CHUNKS) for g in range(PASSES)]
            else:
                steps = [(c, g) for g in range(PASSES) for c in range(OUT_CHUNKS)]
            if u == UNITS - 1:
                sum_late(23, "vector")
                nc.vector.tensor_reduce(
                    out=partial[:], in_=col_sum[:, :, 0:u], axis=mybir.AxisListType.X, op=ALU.add
                )
                nc.vector.tensor_scalar(
                    out=partial[:], in0=partial[:], scalar1=1.0 / ROWS, scalar2=None, op0=ALU.mult
                )
            for c in range(OUT_CHUNKS):
                acc_banks[u, c] = acc[c]
            for c, g in steps:
                nc.tensor.matmul_mx(
                    out=acc[c][:],
                    lhsT=w_words[:, g, 2 * P * c : 2 * P * (c + 1)].bitcast(FP4X4),
                    lhsT_scale=w_scales[:, g, P * c : P * (c + 1)],
                    rhs=words[:, g, :].bitcast(FP8X4),
                    rhs_scale=scales[:, g, :],
                    start=(g == 0),
                    stop=(g == PASSES - 1),
                )
                if g == PASSES - 1 and u == UNITS - 2 and c == 0:
                    quantise(u + 1, 0)
                if g == PASSES - 1 and (u, c) not in later:
                    empty_bank(u, c)

        def empty_bank(u, c):
            bank = acc_banks[u, c]
            if by_vector(u, c):
                nc.vector.scalar_tensor_tensor(
                    out=vj_t[u][:, c, :],
                    in0=bank[:],
                    scalar=b_col[:, c : c + 1],
                    in1=zeros[:],
                    op0=ALU.add,
                    op1=ALU.max,
                    accum_out=col_sum[:, c, u : u + 1],
                )
                if u == UNITS - 1:
                    nc.vector.tensor_scalar(
                        out=repeated[:, c, :],
                        in0=col_sum[:, c, u : u + 1].to_broadcast([P, P]),
                        scalar1=1.0 / ROWS,
                        scalar2=partial[:, c : c + 1],
                        op0=ALU.mult,
                        op1=ALU.add,
                    )
            else:
                nc.scalar.activation(
                    out=vj_t[u][:, c, :],
                    in_=bank[:],
                    func=ACT.Relu,
                    bias=b_col[:, c : c + 1],
                    scale=1.0,
                    accum_out=col_sum[:, c, u : u + 1],
                )
                if u == UNITS - 1:
                    nc.scalar.activation(
                        out=repeated[:, c, :],
                        in_=col_sum[:, c, u : u + 1].to_broadcast([P, P]),
                        func=ACT.Identity,
                        bias=partial[:, c : c + 1],
                        scale=1.0 / ROWS,
                    )

        sum_first_tile()
        sort_and_sum(0)
        transpose_in(0)
        nc.scalar.copy(out=b_rows_f32[:], in_=b_rows[:])
        sort_and_sum(1)
        fold_on_gpsimd(3, work.tile([P, K // 2], F32, name="fold", tag="correction"))
        quantise(0)
        for i in range(UNITS):
            if i + 3 < UNITS:
                load(i + 3)
            if i + 2 < UNITS:
                sort_and_sum(i + 2)
                if i + 2 >= UNITS - LATE_UNITS:
                    sort_late_held(i + 2)
                elif True:
                    sort_held_on_gpsimd(i + 2)
            if i + 1 < UNITS:
                transpose_in(i + 1)
            if i == 0:
                bias_to_partitions()
            if i >= UNITS - 4 and i < UNITS - 1:
                sum_late((i - UNITS + 5) * UNIT_TILES + SORTED_TILES, "vector")
            if i == UNITS - 1:
                sum_late(19, "scalar")
                sum_folded(3)
            multiply(i)
            if i + 1 < UNITS:
                quantise(i + 1, 1)
            if (i, 2) in later:
                empty_bank(i, 2)

        banks = {}
        results = {}

        def transpose_back(t):
            u, j = divmod(t, UNIT_TILES)
            banks[t] = psum.tile([P, OUTS], F32, name="vj", tag="xt" if len(banks) % 2 == 0 else "acc")
            for c in range(OUT_CHUNKS):
                block = vj_t[u][:, c, j * P : (j + 1) * P]
                if c == 0 and t % 3 != 2:
                    nc.tensor.matmul(
                        banks[t][:, c * P : (c + 1) * P], lhsT=block, rhs=ident[:], start=True, stop=True
                    )
                else:
                    nc.tensor.transpose(banks[t][:, c * P : (c + 1) * P], block, ident[:])

        def finish_by_vector(t, cols=slice(0, OUTS)):
            u, j = divmod(t, UNIT_TILES)
            nc.vector.scalar_tensor_tensor(
                out=results[u][:, j, cols],
                in0=mc_all[:, cols],
                scalar=row_sum[:, t : t + 1],
                in1=banks[t][:, cols],
                op0=ALU.mult,
                op1=ALU.add,
            )

        def finish_by_scalar_and_gpsimd(t):
            u, j = divmod(t, UNIT_TILES)
            correction = work.tile([P, OUTS], F32, name="correction")
            if u in (3, 5, 7, 9, 11, 13):
                nc.gpsimd.tensor_scalar(
                    out=correction[:],
                    in0=mc_all[:],
                    scalar1=row_sum[:, t : t + 1],
                    scalar2=0.0,
                    op0=ALU.mult,
                    op1=ALU.add,
                )
            else:
                nc.scalar.activation(
                    out=correction[:], in_=mc_all[:], func=ACT.Copy, scale=row_sum[:, t : t + 1]
                )
            nc.scalar.copy(out=results[u][:, j, :], in_=banks[t][:])
            nc.gpsimd.tensor_tensor(
                out=results[u][:, j, :], in0=results[u][:, j, :], in1=correction[:], op=ALU.add
            )

        def store(first, n, cols=slice(0, OUTS)):
            u, j = divmod(first, UNIT_TILES)
            nc.sync.dma_start(
                out=out_tiles[:, first : first + n, cols], in_=results[u][:, j : j + n, cols]
            )

        mc_all = const.tile([P, OUTS], F32)
        order = list(range(UNIT_TILES))
        for u in range(1, UNITS):
            order.insert(len(order) - (UNIT_TILES - 1 if u > 1 else 2), u * UNIT_TILES + SORTED_TILES)
            order.extend(range(u * UNIT_TILES, u * UNIT_TILES + SORTED_TILES))
        by_gpsimd = set(u * UNIT_TILES + SORTED_TILES for u in range(1, UNITS))

        transpose_back(0)
        halves = []
        for half in range(2):
            m_ps = psum.tile([P, OUTS // 2], F32, name="m_ps", tag="xt" if half == 0 else "acc")
            for c in range(2):
                nc.tensor.transpose(m_ps[:, c * P : (c + 1) * P], repeated[:, 2 * half + c, :], ident[:])
            halves.append(m_ps)
            if half == 0:
                transpose_back(order[1])
        nc.vector.tensor_scalar(
            out=mc_all[:, 0 : OUTS // 2], in0=halves[0][:], scalar1=C, scalar2=None, op0=ALU.mult
        )
        nc.scalar.mul(out=mc_all[:, OUTS // 2 : OUTS], in_=halves[1][:], mul=C)
        for t in order[2:LOOKAHEAD]:
            transpose_back(t)

        stores = {2: [(2, 1)], 3: [(3, 1)]}
        for u in range(1, UNITS):
            first = u * UNIT_TILES
            if u < SMALL_STORE_UNITS:
                stores[first] = [(first, 1)]
                stores[first + 1] = [(first + 1, 1)]
                stores[first + 2] = [(first + 2, 2)]
            elif u < HALVES:
                stores[first + 1] = [(first, 2)]
                stores[first + 2] = [(first + 2, 2)]
            elif u < UNITS - 1:
                stores[first + 2] = [(first, UNIT_TILES)]
            else:
                stores[first + 1] = [(first, 2), (first + 3, 1)]
                stores[first + 2] = [(first + 2, 1)]
        unsummed = [
            u * UNIT_TILES + j for u in range(UNITS - LATE_UNITS, UNITS) for j in range(SORTED_TILES)
        ]
        vector_sums = {5 + n: t for n, t in enumerate(unsummed)}
        for n, t in enumerate(order):
            u, j = divmod(t, UNIT_TILES)
            if n + LOOKAHEAD < TILES:
                transpose_back(order[n + LOOKAHEAD])
            if u not in results and u < 2:
                results[u] = work.tile([P, UNIT_TILES, OUTS], F32, name="result", tag="grouped", align_bytes=64)
            elif u not in results:
                results[u] = keep.tile([P, UNIT_TILES, OUTS], F32, name="result", tag="unit_f32")
            if t in by_gpsimd:
                if u in {3: 18, 5: 30, 7: 42, 9: 50}:
                    sum_late({3: 18, 5: 30, 7: 42, 9: 50}[u], "scalar")
                if u > 5:
                    sum_late(t, "scalar")
                finish_by_scalar_and_gpsimd(t)
            elif n == 0:
                for half in range(2):
                    cols = slice(half * OUTS // 2, (half + 1) * OUTS // 2)
                    for first in range(EARLY):
                        finish_by_vector(first, cols)
                        store(first, 1, cols)
            elif n >= EARLY:
                finish_by_vector(t)
            if j == UNIT_TILES - 2 and u in vector_sums:
                sum_late(vector_sums[u], "vector")
            for first, count in stores.get(t, []):
                store(first, count)
            if n == 2:
                m_all = work.tile([P, OUTS], F32, name="m_all", tag="x_sorted")
                for half in range(2):
                    nc.scalar.copy(
                        out=m_all[:, half * OUTS // 2 : (half + 1) * OUTS // 2], in_=halves[half][:]
                    )
            if n == 12:
                nc.sync.dma_start(out=out_1.rearrange("(a o) -> a o", a=1), in_=m_all[0:1, :])
